import numpy as np
import ml_dtypes


def mxq(x, axis, fmt="e4m3"):
    dtype, down = {"e4m3": (ml_dtypes.float8_e4m3fn, 7), "e5m2": (ml_dtypes.float8_e5m2, 14)}[fmt]
    v = np.moveaxis(np.asarray(x, np.float32).astype(ml_dtypes.bfloat16).astype(np.float64), axis, -1)
    blocks = v.reshape(v.shape[:-1] + (-1, 32))
    amax = np.abs(blocks).max(-1, keepdims=True)
    byte = np.maximum(np.where(amax > 0, np.frexp(amax)[1] - 1 + 127, 0) - down, 1)
    scale = np.exp2(byte - 127.0)
    codes = (blocks / scale).astype(np.float32).astype(dtype).astype(np.float64)
    return np.moveaxis((codes * scale).reshape(v.shape), -1, axis)


WIDE = False


def mx_kscale(k):
    if not WIDE:
        return np.ones(k)
    levels = np.array([10, -10, 5, -5, 0])
    a = np.random.permutation(np.resize(levels, k // 512 * 4)).reshape(k // 512, 4)
    idx = np.arange(k)
    return np.exp2(a[idx // 512, idx % 128 // 32])


BF16 = ml_dtypes.bfloat16


def bf(x):
    return np.asarray(x, np.float32).astype(BF16)


def f64(x):
    return np.asarray(x).astype(np.float64)


E2M1 = np.array([0.0, 0.5, 1.0, 1.5, 2.0, 3.0, 4.0, 6.0, -0.0, -0.5, -1.0, -1.5, -2.0, -3.0, -4.0, -6.0])


def pack_weight(w, fmt):
    k, n = w.shape
    w = f64(bf(w)).reshape(k // 32, 32, n)
    amax = np.abs(w).max(1)
    if fmt == "e4m3":
        byte = np.frexp(amax)[1] - 1 + 127 - 7
    else:
        mant, ex = np.frexp(amax / 6.0)
        byte = np.where(mant > 0.5, ex, ex - 1) + 127
    byte = np.clip(np.where(amax > 0, byte, 1), 1, 254)
    scaled = (w * np.exp2(127.0 - byte)[:, None, :]).reshape(k, n).astype(np.float32)
    by_word = np.ascontiguousarray(scaled.reshape(k // 512, 128, 4, n).transpose(0, 1, 3, 2))
    if fmt == "e4m3":
        words = by_word.astype(ml_dtypes.float8_e4m3fn).view(np.uint8)
    else:
        c = by_word.astype(ml_dtypes.float4_e2m1fn).view(np.uint8) & 0xF
        words = c[..., 0::2] | (c[..., 1::2] << 4)
    return np.ascontiguousarray(words), np.ascontiguousarray(byte.astype(np.uint8).reshape(k // 512, 16, n))


def unpack_weight(words, scales, fmt):
    g, p, n, _ = words.shape
    if fmt == "e4m3":
        vals = np.ascontiguousarray(words).view(ml_dtypes.float8_e4m3fn).astype(np.float64)
    else:
        nib = np.empty((g, p, n, 4), np.uint8)
        nib[..., 0::2] = words & 0xF
        nib[..., 1::2] = words >> 4
        vals = E2M1[nib]
    vals = vals * np.repeat(np.exp2(scales.astype(np.float64) - 127.0), 8, axis=1)[..., None]
    return vals.transpose(0, 1, 3, 2).reshape(g * 512, n)


B, S, DV, D, H, A = 4, 1024, 1024, 256, 2, 64
LN_EPS = 1e-3


def setup_inputs():
    s = mx_kscale(DV)
    attn = bf(np.random.standard_normal((B, H, S, DV)) * 0.4 * s)
    Wo = np.random.standard_normal((H, DV, D)) * 0.6 / np.sqrt(DV * H) / s[None, :, None]
    Wo_words, Wo_scales = pack_weight(Wo.reshape(-1, D), "e4m3")
    return {
        "attn": attn,
        "Wo_words": Wo_words,
        "Wo_scales": Wo_scales,
        "bo": bf(np.random.standard_normal((H, D)) * 0.12 / np.sqrt(H)),
        "query_inputs": bf(np.random.standard_normal((B, S, D)) * 0.1),
        "gamma": bf(1.0 + 0.1 * np.random.standard_normal(D)),
        "beta": bf(0.1 * np.random.standard_normal(D)),
    }


def reference(attn, Wo_words, Wo_scales, bo, query_inputs, gamma, beta):
    pre = mxq(f64(attn), 3, "e4m3") @ unpack_weight(Wo_words, Wo_scales, "e4m3").reshape(H, DV, D)
    head_out = np.maximum(pre + f64(bo)[None, :, None, :], 0.0)
    x = f64(query_inputs) + head_out.sum(axis=1)
    mean = x.mean(axis=-1, keepdims=True)
    var = x.var(axis=-1, keepdims=True)
    return f64(gamma) * (x - mean) / np.sqrt(var + LN_EPS) + f64(beta)

@@ -1,0 +1,267 @@
+from contextlib import ExitStack
+
+import concourse.mybir as mybir
+from concourse.masks import make_identity
+
+F32 = mybir.dt.float32
+BF16 = mybir.dt.bfloat16
+I32 = mybir.dt.int32
+U32 = mybir.dt.uint32
+U8 = mybir.dt.uint8
+FP8X4 = mybir.dt.float8_e4m3fn_x4
+ALU = mybir.AluOpType
+ACT = mybir.ActivationFunctionType
+
+B, H, S, DV, D = 4, 2, 1024, 1024, 256
+LN_EPS = 1e-3
+FLOPS = 2 * B * H * S * DV * D
+
+P = 128
+K_PASS = 4 * P
+PASSES = DV // K_PASS
+PAIRS = 2
+ROW_TILES = 4
+UNIT_ROWS = P * ROW_TILES
+UNITS = B * S // UNIT_ROWS
+STEPS = UNITS * H
+D_HALVES = D // P
+HALF_TILES = ROW_TILES // 2
+HALVES = UNITS * 2
+HALF_ROWS = P * HALF_TILES
+PREFETCH = 6
+
+
+def tile_multiheadattentionunit_pa_t_e_kernel(
+    tc, attn, Wo_words, Wo_scales, bo, query_inputs, gamma, beta, out
+):
+    nc = tc.nc
+    with ExitStack() as stack:
+        consts = stack.enter_context(tc.tile_pool(name="consts", bufs=1))
+        attn_pool = stack.enter_context(tc.tile_pool(name="attn_pool", bufs=PREFETCH + 1))
+        resid_pool = stack.enter_context(tc.tile_pool(name="resid_pool", bufs=4))
+        quant_pool = stack.enter_context(tc.tile_pool(name="quant_pool", bufs=3))
+        head_pool = stack.enter_context(tc.tile_pool(name="head_pool", bufs=4))
+        norm_pool = stack.enter_context(tc.tile_pool(name="norm_pool", bufs=3))
+        fwd_psum = stack.enter_context(tc.psum_pool(name="fwd_psum", bufs=4))
+        acc_psum = stack.enter_context(tc.psum_pool(name="acc_psum", bufs=2))
+        back_psum = stack.enter_context(tc.psum_pool(name="back_psum", bufs=2))
+        stack.enter_context(tc.manual_schedule())
+
+        attn_tiles, resid_tiles, grouped_tiles, code_tiles, scale_tiles = {}, {}, {}, {}, {}
+        relu_tiles, sum_tiles, back_tiles, x_tiles, negmean_tiles, std_tiles = {}, {}, {}, {}, {}, {}
+
+        def load_attn(step):
+            unit, h = step // H, step % H
+            b, row0 = unit * UNIT_ROWS // S, unit * UNIT_ROWS % S
+            x_rows = attn_pool.tile([P, ROW_TILES, DV], BF16)
+            nc.sync.dma_start(
+                out=x_rows[:],
+                in_=attn[b, h, row0 : row0 + UNIT_ROWS, :].rearrange("(p j) k -> p j k", j=ROW_TILES),
+            )
+            attn_tiles[step] = x_rows
+
+        def load_residual(unit):
+            b, row0 = unit * UNIT_ROWS // S, unit * UNIT_ROWS % S
+            resid = resid_pool.tile([P, ROW_TILES, D], BF16)
+            nc.sync.dma_start(
+                out=resid[:],
+                in_=query_inputs[b, row0 : row0 + UNIT_ROWS, :].rearrange("(p j) d -> p j d", j=ROW_TILES),
+            )
+            resid_tiles[unit] = resid
+
+        load_attn(0)
+
+        w_words = consts.tile([P, H * PASSES, D], U32, align_bytes=64)
+        nc.sync.dma_start(
+            out=w_words[:].bitcast(I32),
+            in_=Wo_words.rearrange("c p n t -> p c (n t)").bitcast(I32),
+        )
+        w_scales = consts.tile([P, H * PASSES, D], U8, align_bytes=64)
+        nc.vector.memset(w_scales[:].rearrange("p c n -> p (c n)").bitcast(I32), 0)
+        for quadrant in range(4):
+            nc.sync.dma_start(
+                out=w_scales[32 * quadrant : 32 * quadrant + 4, :, :].bitcast(I32),
+                in_=Wo_scales.bitcast(I32)[:, 4 * quadrant : 4 * quadrant + 4, :].rearrange("c r n -> r c n"),
+            )
+        for step in range(1, PREFETCH):
+            load_attn(step)
+
+        ident = consts.tile([P, P], F32)
+        make_identity(nc, ident[:])
+        ones = consts.tile([P, P], BF16)
+        nc.vector.memset(ones[:], 1.0)
+
+        affine_rows = consts.tile([P, 2 * D], BF16)
+        nc.vector.memset(affine_rows[:], 0.0)
+        nc.scalar.dma_start(out=affine_rows[0:1, 0:D], in_=gamma.rearrange("(o d) -> o d", o=1))
+        nc.scalar.dma_start(out=affine_rows[0:1, D : 2 * D], in_=beta.rearrange("(o d) -> o d", o=1))
+        bias_rows = consts.tile([P, P], BF16)
+        nc.vector.memset(bias_rows[:], 0.0)
+        nc.scalar.dma_start(
+            out=bias_rows[0 : H * D_HALVES, :], in_=bo.rearrange("h (c d) -> (h c) d", c=D_HALVES)
+        )
+        warm = consts.tile([P, 1], F32)
+        nc.scalar.activation(out=warm[:], in_=ones[:, 0:1], func=ACT.Sqrt)
+
+        spread = acc_psum.tile([P, UNIT_ROWS], F32, tag="acc")
+        nc.tensor.matmul(out=spread[:], lhsT=ones[:], rhs=affine_rows[:], start=True, stop=True)
+        affine = consts.tile([P, 2 * D], F32)
+        nc.vector.tensor_copy(out=affine[:], in_=spread[:])
+        gamma_all, beta_all = affine[:, 0:D], affine[:, D : 2 * D]
+
+        bias_rows_f32 = consts.tile([P, P], F32)
+        nc.vector.tensor_copy(out=bias_rows_f32[:], in_=bias_rows[:])
+        bias_psum = back_psum.tile([P, HALF_TILES, D], F32, tag="back")
+        nc.tensor.transpose(bias_psum[:, 0, 0:P], bias_rows_f32[:], ident[:])
+        bias_cols = consts.tile([P, H * D_HALVES], F32)
+        nc.vector.tensor_copy(out=bias_cols[:], in_=bias_psum[:, 0, 0 : H * D_HALVES])
+
+        def transpose(step):
+            x_rows = attn_tiles[step]
+            grouped = quant_pool.tile([P, PASSES, UNIT_ROWS, 4], BF16, align_bytes=64)
+            grouped_words = grouped[:].bitcast(F32)
+            for j in range(ROW_TILES):
+                words = x_rows[:, j, :].bitcast(F32)
+                flipped = fwd_psum.tile([P, PASSES, PAIRS, P], F32)
+                for g in range(PASSES):
+                    for u in range(PAIRS):
+                        first = g * K_PASS // 2 + u
+                        nc.tensor.transpose(
+                            flipped[:, g, u, :], words[:, first : (g + 1) * K_PASS // 2 : PAIRS], ident[:]
+                        )
+                nc.scalar.copy(
+                    out=grouped_words[:, :, j * P : (j + 1) * P, :],
+                    in_=flipped[:].rearrange("p g u r -> p g r u"),
+                )
+            grouped_tiles[step] = grouped
+
+        def quantise(step):
+            codes = quant_pool.tile([P, PASSES, UNIT_ROWS], U32, align_bytes=64)
+            scales = quant_pool.tile([P, PASSES, UNIT_ROWS], U8, align_bytes=64)
+            nc.vector.quantize_mx(
+                out=codes[:].rearrange("p g c -> p (g c)").bitcast(FP8X4),
+                scales=scales[:].rearrange("p g c -> p (g c)"),
+                in_=grouped_tiles[step][:].rearrange("p g c t -> p (g c t)"),
+            )
+            code_tiles[step], scale_tiles[step] = codes, scales
+
+        def multiply(step):
+            h = step % H
+            codes, scales = code_tiles[step], scale_tiles[step]
+            relu = head_pool.tile([P, D_HALVES, UNIT_ROWS], F32)
+            for c in range(D_HALVES):
+                acc = acc_psum.tile([P, UNIT_ROWS], F32)
+                for g in range(PASSES):
+                    nc.tensor.matmul_mx(
+                        out=acc[:],
+                        lhsT=w_words[:, h * PASSES + g, c * P : (c + 1) * P].bitcast(FP8X4),
+                        lhsT_scale=w_scales[:, h * PASSES + g, c * P : (c + 1) * P],
+                        rhs=codes[:, g, :].bitcast(FP8X4),
+                        rhs_scale=scales[:, g, :],
+                        start=(g == 0),
+                        stop=(g == PASSES - 1),
+                    )
+                column = h * D_HALVES + c
+                nc.scalar.activation(
+                    out=relu[:, c, :], in_=acc[:], func=ACT.Relu, bias=bias_cols[:, column : column + 1], scale=1.0
+                )
+            relu_tiles[step] = relu
+
+        def sum_heads(half):
+            unit, cols = half // 2, slice(half % 2 * HALF_ROWS, (half % 2 + 1) * HALF_ROWS)
+            heads = norm_pool.tile([P, D_HALVES, HALF_ROWS], F32)
+            nc.vector.tensor_add(
+                out=heads[:], in0=relu_tiles[unit * H][:, :, cols], in1=relu_tiles[unit * H + 1][:, :, cols]
+            )
+            sum_tiles[half] = heads
+
+        def back_transpose(half):
+            heads = sum_tiles[half]
+            back = back_psum.tile([P, HALF_TILES, D], F32)
+            for i in range(HALF_TILES):
+                for c in range(D_HALVES):
+                    nc.tensor.transpose(
+                        back[:, i, c * P : (c + 1) * P], heads[:, c, i * P : (i + 1) * P], ident[:]
+                    )
+            back_tiles[half] = back
+
+        def add_residual(half):
+            back, resid = back_tiles[half], resid_tiles[half // 2]
+            x = norm_pool.tile([P, HALF_TILES, D], F32)
+            rowsum = norm_pool.tile([P, HALF_TILES], F32)
+            for i in range(HALF_TILES):
+                nc.vector.scalar_tensor_tensor(
+                    out=x[:, i, :],
+                    in0=back[:, i, :],
+                    scalar=1.0,
+                    in1=resid[:, half % 2 * HALF_TILES + i, :],
+                    op0=ALU.mult,
+                    op1=ALU.add,
+                    accum_out=rowsum[:, i : i + 1],
+                )
+            negmean = norm_pool.tile([P, HALF_TILES], F32)
+            nc.vector.tensor_scalar_mul(out=negmean[:], in0=rowsum[:], scalar1=-1.0 / D)
+            x_tiles[half], negmean_tiles[half] = x, negmean
+
+        def deviation(half):
+            x, negmean = x_tiles[half], negmean_tiles[half]
+            squares = norm_pool.tile([P, HALF_TILES, D], F32)
+            sumsq = norm_pool.tile([P, HALF_TILES], F32)
+            for i in range(HALF_TILES):
+                nc.scalar.activation(
+                    out=squares[:, i, :],
+                    in_=x[:, i, :],
+                    func=ACT.Square,
+                    bias=negmean[:, i : i + 1],
+                    scale=1.0,
+                    accum_out=sumsq[:, i : i + 1],
+                )
+            std = norm_pool.tile([P, HALF_TILES], F32)
+            nc.scalar.activation(out=std[:], in_=sumsq[:], func=ACT.Sqrt, bias=LN_EPS, scale=1.0 / D)
+            std_tiles[half] = std
+
+        def normalise(half):
+            x, negmean = x_tiles[half], negmean_tiles[half]
+            unit = half // 2
+            b, row0 = unit * UNIT_ROWS // S, unit * UNIT_ROWS % S
+            scaled = norm_pool.tile([P, HALF_TILES, D], F32)
+            for i in range(HALF_TILES):
+                nc.vector.scalar_tensor_tensor(
+                    out=scaled[:, i, :], in0=x[:, i, :], scalar=negmean[:, i : i + 1], in1=gamma_all,
+                    op0=ALU.add, op1=ALU.mult,
+                )
+            rstd = norm_pool.tile([P, HALF_TILES], F32)
+            nc.vector.reciprocal(out=rstd[:], in_=std_tiles[half][:])
+            result = norm_pool.tile([P, HALF_TILES, D], F32)
+            for i in range(HALF_TILES):
+                nc.vector.scalar_tensor_tensor(
+                    out=result[:, i, :], in0=scaled[:, i, :], scalar=rstd[:, i : i + 1], in1=beta_all,
+                    op0=ALU.mult, op1=ALU.add,
+                )
+            tiles = slice(half % 2 * HALF_TILES, (half % 2 + 1) * HALF_TILES)
+            nc.sync.dma_start(
+                out=out[b, row0 : row0 + UNIT_ROWS, :].rearrange("(p j) d -> p j d", j=ROW_TILES)[:, tiles, :],
+                in_=result[:],
+            )
+
+        for i in range(HALVES + 4):
+            if i + PREFETCH < STEPS:
+                load_attn(i + PREFETCH)
+            if i % H == 0 and i // H < UNITS:
+                load_residual(i // H)
+            if 0 <= i - 1 < STEPS:
+                quantise(i - 1)
+            if 0 <= i - 3 < HALVES:
+                sum_heads(i - 3)
+            if 0 <= i - 4 < HALVES:
+                deviation(i - 4)
+            if i < STEPS:
+                transpose(i)
+            if 0 <= i - 3 < HALVES:
+                back_transpose(i - 3)
+            if 0 <= i - 1 < STEPS:
+                multiply(i - 1)
+            if 0 <= i - 4 < HALVES:
+                normalise(i - 4)
+            if 0 <= i - 3 < HALVES:
+                add_residual(i - 3)

@@ -20,15 +20,12 @@ P = 128
 K_PASS = 4 * P
 PASSES = DV // K_PASS
 PAIRS = 2
-ROW_TILES = 4
+ROW_TILES = 2
 UNIT_ROWS = P * ROW_TILES
 UNITS = B * S // UNIT_ROWS
-STEPS = UNITS * H
 D_HALVES = D // P
-HALF_TILES = ROW_TILES // 2
-HALVES = UNITS * 2
-HALF_ROWS = P * HALF_TILES
 PREFETCH = 6
+CONSTANTS_ROUND = 0
 
 
 def tile_multiheadattentionunit_pa_t_e_kernel(
@@ -37,9 +34,8 @@ def tile_multiheadattentionunit_pa_t_e_kernel(
     nc = tc.nc
     with ExitStack() as stack:
         consts = stack.enter_context(tc.tile_pool(name="consts", bufs=1))
-        attn_pool = stack.enter_context(tc.tile_pool(name="attn_pool", bufs=PREFETCH + 1))
+        attn_pool = stack.enter_context(tc.tile_pool(name="attn_pool", bufs=H * (PREFETCH + 1)))
         resid_pool = stack.enter_context(tc.tile_pool(name="resid_pool", bufs=4))
-        quant_pool = stack.enter_context(tc.tile_pool(name="quant_pool", bufs=3))
         head_pool = stack.enter_context(tc.tile_pool(name="head_pool", bufs=4))
         norm_pool = stack.enter_context(tc.tile_pool(name="norm_pool", bufs=3))
         fwd_psum = stack.enter_context(tc.psum_pool(name="fwd_psum", bufs=4))
@@ -47,25 +43,27 @@ def tile_multiheadattentionunit_pa_t_e_kernel(
         back_psum = stack.enter_context(tc.psum_pool(name="back_psum", bufs=2))
         stack.enter_context(tc.manual_schedule())
 
-        attn_tiles, resid_tiles, grouped_tiles, code_tiles, scale_tiles = {}, {}, {}, {}, {}
-        relu_tiles, sum_tiles, back_tiles, x_tiles, negmean_tiles, std_tiles = {}, {}, {}, {}, {}, {}
+        attn_tiles, grouped_tiles, code_tiles, scale_tiles, relu_tiles = {}, {}, {}, {}, {}
+        resid_tiles, sum_tiles, back_tiles, x_tiles, rowsum_tiles = {}, {}, {}, {}, {}
+        negmean_tiles, rstd_tiles, scaled_tiles = {}, {}, {}
 
-        def load_attn(step):
-            unit, h = step // H, step % H
-            b, row0 = unit * UNIT_ROWS // S, unit * UNIT_ROWS % S
-            x_rows = attn_pool.tile([P, ROW_TILES, DV], BF16)
-            nc.sync.dma_start(
-                out=x_rows[:],
-                in_=attn[b, h, row0 : row0 + UNIT_ROWS, :].rearrange("(p j) k -> p j k", j=ROW_TILES),
-            )
-            attn_tiles[step] = x_rows
+        def rows_of(unit):
+            return unit * UNIT_ROWS // S, slice(unit * UNIT_ROWS % S, unit * UNIT_ROWS % S + UNIT_ROWS)
+
+        def load_attn(unit):
+            b, rows = rows_of(unit)
+            for h in range(H):
+                x_rows = attn_pool.tile([P, ROW_TILES, DV], BF16)
+                nc.sync.dma_start(
+                    out=x_rows[:], in_=attn[b, h, rows, :].rearrange("(p j) k -> p j k", j=ROW_TILES)
+                )
+                attn_tiles[unit, h] = x_rows
 
         def load_residual(unit):
-            b, row0 = unit * UNIT_ROWS // S, unit * UNIT_ROWS % S
+            b, rows = rows_of(unit)
             resid = resid_pool.tile([P, ROW_TILES, D], BF16)
             nc.sync.dma_start(
-                out=resid[:],
-                in_=query_inputs[b, row0 : row0 + UNIT_ROWS, :].rearrange("(p j) d -> p j d", j=ROW_TILES),
+                out=resid[:], in_=query_inputs[b, rows, :].rearrange("(p j) d -> p j d", j=ROW_TILES)
             )
             resid_tiles[unit] = resid
 
@@ -83,13 +81,15 @@ def tile_multiheadattentionunit_pa_t_e_kernel(
                 out=w_scales[32 * quadrant : 32 * quadrant + 4, :, :].bitcast(I32),
                 in_=Wo_scales.bitcast(I32)[:, 4 * quadrant : 4 * quadrant + 4, :].rearrange("c r n -> r c n"),
             )
-        for step in range(1, PREFETCH):
-            load_attn(step)
+        for unit in range(1, PREFETCH):
+            load_attn(unit)
 
         ident = consts.tile([P, P], F32)
         make_identity(nc, ident[:])
         ones = consts.tile([P, P], BF16)
         nc.vector.memset(ones[:], 1.0)
+        neg_half = consts.tile([P, ROW_TILES], F32)
+        nc.vector.memset(neg_half[:], -0.5)
 
         affine_rows = consts.tile([P, 2 * D], BF16)
         nc.vector.memset(affine_rows[:], 0.0)
@@ -100,25 +100,25 @@ def tile_multiheadattentionunit_pa_t_e_kernel(
         nc.scalar.dma_start(
             out=bias_rows[0 : H * D_HALVES, :], in_=bo.rearrange("h (c d) -> (h c) d", c=D_HALVES)
         )
-        warm = consts.tile([P, 1], F32)
-        nc.scalar.activation(out=warm[:], in_=ones[:, 0:1], func=ACT.Sqrt)
-
-        spread = acc_psum.tile([P, UNIT_ROWS], F32, tag="acc")
-        nc.tensor.matmul(out=spread[:], lhsT=ones[:], rhs=affine_rows[:], start=True, stop=True)
         affine = consts.tile([P, 2 * D], F32)
-        nc.vector.tensor_copy(out=affine[:], in_=spread[:])
         gamma_all, beta_all = affine[:, 0:D], affine[:, D : 2 * D]
-
         bias_rows_f32 = consts.tile([P, P], F32)
-        nc.vector.tensor_copy(out=bias_rows_f32[:], in_=bias_rows[:])
-        bias_psum = back_psum.tile([P, HALF_TILES, D], F32, tag="back")
-        nc.tensor.transpose(bias_psum[:, 0, 0:P], bias_rows_f32[:], ident[:])
         bias_cols = consts.tile([P, H * D_HALVES], F32)
-        nc.vector.tensor_copy(out=bias_cols[:], in_=bias_psum[:, 0, 0 : H * D_HALVES])
 
-        def transpose(step):
-            x_rows = attn_tiles[step]
-            grouped = quant_pool.tile([P, PASSES, UNIT_ROWS, 4], BF16, align_bytes=64)
+        def spread_constants():
+            spread = acc_psum.tile([P, D_HALVES, UNIT_ROWS], F32, tag="acc")
+            nc.tensor.matmul(
+                out=spread[:].rearrange("p c r -> p (c r)"), lhsT=ones[:], rhs=affine_rows[:], start=True, stop=True
+            )
+            nc.vector.tensor_copy(out=affine[:], in_=spread[:].rearrange("p c r -> p (c r)"))
+            nc.vector.tensor_copy(out=bias_rows_f32[:], in_=bias_rows[:])
+            bias_psum = back_psum.tile([P, ROW_TILES, D], F32, tag="back")
+            nc.tensor.transpose(bias_psum[:, 0, 0:P], bias_rows_f32[:], ident[:])
+            nc.vector.tensor_copy(out=bias_cols[:], in_=bias_psum[:, 0, 0 : H * D_HALVES])
+
+        def transpose(unit, h):
+            x_rows = attn_tiles[unit, h]
+            grouped = head_pool.tile([P, PASSES, UNIT_ROWS, 4], BF16, align_bytes=64)
             grouped_words = grouped[:].bitcast(F32)
             for j in range(ROW_TILES):
                 words = x_rows[:, j, :].bitcast(F32)
@@ -133,27 +133,26 @@ def tile_multiheadattentionunit_pa_t_e_kernel(
                     out=grouped_words[:, :, j * P : (j + 1) * P, :],
                     in_=flipped[:].rearrange("p g u r -> p g r u"),
                 )
-            grouped_tiles[step] = grouped
+            grouped_tiles[unit, h] = grouped
 
-        def quantise(step):
-            codes = quant_pool.tile([P, PASSES, UNIT_ROWS], U32, align_bytes=64)
-            scales = quant_pool.tile([P, PASSES, UNIT_ROWS], U8, align_bytes=64)
+        def quantise(unit, h):
+            codes = head_pool.tile([P, PASSES, UNIT_ROWS], U32, align_bytes=64)
+            scales = head_pool.tile([P, PASSES, UNIT_ROWS], U8, align_bytes=64)
             nc.vector.quantize_mx(
                 out=codes[:].rearrange("p g c -> p (g c)").bitcast(FP8X4),
                 scales=scales[:].rearrange("p g c -> p (g c)"),
-                in_=grouped_tiles[step][:].rearrange("p g c t -> p (g c t)"),
+                in_=grouped_tiles[unit, h][:].rearrange("p g c t -> p (g c t)"),
             )
-            code_tiles[step], scale_tiles[step] = codes, scales
+            code_tiles[unit, h], scale_tiles[unit, h] = codes, scales
 
-        def multiply(step):
-            h = step % H
-            codes, scales = code_tiles[step], scale_tiles[step]
+        def multiply(unit, h):
+            codes, scales = code_tiles[unit, h], scale_tiles[unit, h]
             relu = head_pool.tile([P, D_HALVES, UNIT_ROWS], F32)
+            acc = acc_psum.tile([P, D_HALVES, UNIT_ROWS], F32)
             for c in range(D_HALVES):
-                acc = acc_psum.tile([P, UNIT_ROWS], F32)
                 for g in range(PASSES):
                     nc.tensor.matmul_mx(
-                        out=acc[:],
+                        out=acc[:, c, :],
                         lhsT=w_words[:, h * PASSES + g, c * P : (c + 1) * P].bitcast(FP8X4),
                         lhsT_scale=w_scales[:, h * PASSES + g, c * P : (c + 1) * P],
                         rhs=codes[:, g, :].bitcast(FP8X4),
@@ -161,107 +160,125 @@ def tile_multiheadattentionunit_pa_t_e_kernel(
                         start=(g == 0),
                         stop=(g == PASSES - 1),
                     )
+            for c in range(D_HALVES):
                 column = h * D_HALVES + c
                 nc.scalar.activation(
-                    out=relu[:, c, :], in_=acc[:], func=ACT.Relu, bias=bias_cols[:, column : column + 1], scale=1.0
+                    out=relu[:, c, :], in_=acc[:, c, :], func=ACT.Relu,
+                    bias=bias_cols[:, column : column + 1], scale=1.0,
                 )
-            relu_tiles[step] = relu
+            relu_tiles[unit, h] = relu
 
-        def sum_heads(half):
-            unit, cols = half // 2, slice(half % 2 * HALF_ROWS, (half % 2 + 1) * HALF_ROWS)
-            heads = norm_pool.tile([P, D_HALVES, HALF_ROWS], F32)
-            nc.vector.tensor_add(
-                out=heads[:], in0=relu_tiles[unit * H][:, :, cols], in1=relu_tiles[unit * H + 1][:, :, cols]
+        def sum_heads(unit):
+            heads = norm_pool.tile([P, D_HALVES, UNIT_ROWS], F32)
+            nc.vector.tensor_add(out=heads[:], in0=relu_tiles[unit, 0][:], in1=relu_tiles[unit, 1][:])
+            sum_tiles[unit] = heads
+
+        def back_transpose(unit, j):
+            if j == 0:
+                back = back_psum.tile([P, ROW_TILES, D], F32)
+                back_tiles[unit] = back
+            for c in range(D_HALVES):
+                nc.tensor.transpose(
+                    back_tiles[unit][:, j, c * P : (c + 1) * P], sum_tiles[unit][:, c, j * P : (j + 1) * P], ident[:]
+                )
+
+        def add_residual(unit, j):
+            if j == 0:
+                x = norm_pool.tile([P, ROW_TILES, D], F32)
+                rowsum = norm_pool.tile([P, ROW_TILES], F32)
+                x_tiles[unit], rowsum_tiles[unit] = x, rowsum
+            nc.vector.scalar_tensor_tensor(
+                out=x_tiles[unit][:, j, :],
+                in0=back_tiles[unit][:, j, :],
+                scalar=1.0,
+                in1=resid_tiles[unit][:, j, :],
+                op0=ALU.mult,
+                op1=ALU.add,
+                accum_out=rowsum_tiles[unit][:, j : j + 1],
             )
-            sum_tiles[half] = heads
-
-        def back_transpose(half):
-            heads = sum_tiles[half]
-            back = back_psum.tile([P, HALF_TILES, D], F32)
-            for i in range(HALF_TILES):
-                for c in range(D_HALVES):
-                    nc.tensor.transpose(
-                        back[:, i, c * P : (c + 1) * P], heads[:, c, i * P : (i + 1) * P], ident[:]
-                    )
-            back_tiles[half] = back
-
-        def add_residual(half):
-            back, resid = back_tiles[half], resid_tiles[half // 2]
-            x = norm_pool.tile([P, HALF_TILES, D], F32)
-            rowsum = norm_pool.tile([P, HALF_TILES], F32)
-            for i in range(HALF_TILES):
-                nc.vector.scalar_tensor_tensor(
-                    out=x[:, i, :],
-                    in0=back[:, i, :],
-                    scalar=1.0,
-                    in1=resid[:, half % 2 * HALF_TILES + i, :],
-                    op0=ALU.mult,
-                    op1=ALU.add,
-                    accum_out=rowsum[:, i : i + 1],
+            if j == ROW_TILES - 1:
+                negmean = norm_pool.tile([P, ROW_TILES], F32)
+                nc.gpsimd.tensor_scalar(
+                    out=negmean[:], in0=rowsum_tiles[unit][:], scalar1=-1.0 / D, scalar2=0.0, op0=ALU.mult, op1=ALU.add
                 )
-            negmean = norm_pool.tile([P, HALF_TILES], F32)
-            nc.vector.tensor_scalar_mul(out=negmean[:], in0=rowsum[:], scalar1=-1.0 / D)
-            x_tiles[half], negmean_tiles[half] = x, negmean
+                negmean_tiles[unit] = negmean
 
-        def deviation(half):
-            x, negmean = x_tiles[half], negmean_tiles[half]
-            squares = norm_pool.tile([P, HALF_TILES, D], F32)
-            sumsq = norm_pool.tile([P, HALF_TILES], F32)
-            for i in range(HALF_TILES):
+        def deviation(unit):
+            x, negmean = x_tiles[unit], negmean_tiles[unit]
+            squares = norm_pool.tile([P, ROW_TILES, D], F32)
+            sumsq = norm_pool.tile([P, ROW_TILES], F32)
+            for j in range(ROW_TILES):
                 nc.scalar.activation(
-                    out=squares[:, i, :],
-                    in_=x[:, i, :],
+                    out=squares[:, j, :],
+                    in_=x[:, j, :],
                     func=ACT.Square,
-                    bias=negmean[:, i : i + 1],
+                    bias=negmean[:, j : j + 1],
                     scale=1.0,
-                    accum_out=sumsq[:, i : i + 1],
+                    accum_out=sumsq[:, j : j + 1],
                 )
-            std = norm_pool.tile([P, HALF_TILES], F32)
-            nc.scalar.activation(out=std[:], in_=sumsq[:], func=ACT.Sqrt, bias=LN_EPS, scale=1.0 / D)
-            std_tiles[half] = std
+            var_eps = norm_pool.tile([P, ROW_TILES], F32)
+            nc.gpsimd.tensor_scalar(
+                out=var_eps[:], in0=sumsq[:], scalar1=1.0 / D, scalar2=LN_EPS, op0=ALU.mult, op1=ALU.add
+            )
+            rstd = norm_pool.tile([P, ROW_TILES], F32)
+            nc.gpsimd.tensor_tensor(out=rstd[:], in0=var_eps[:], in1=neg_half[:], op=ALU.pow)
+            rstd_tiles[unit] = rstd
 
-        def normalise(half):
-            x, negmean = x_tiles[half], negmean_tiles[half]
-            unit = half // 2
-            b, row0 = unit * UNIT_ROWS // S, unit * UNIT_ROWS % S
-            scaled = norm_pool.tile([P, HALF_TILES, D], F32)
-            for i in range(HALF_TILES):
+        def centre(unit):
+            x, negmean = x_tiles[unit], negmean_tiles[unit]
+            scaled = norm_pool.tile([P, ROW_TILES, D], F32)
+            for j in range(ROW_TILES):
                 nc.vector.scalar_tensor_tensor(
-                    out=scaled[:, i, :], in0=x[:, i, :], scalar=negmean[:, i : i + 1], in1=gamma_all,
+                    out=scaled[:, j, :], in0=x[:, j, :], scalar=negmean[:, j : j + 1], in1=gamma_all,
                     op0=ALU.add, op1=ALU.mult,
                 )
-            rstd = norm_pool.tile([P, HALF_TILES], F32)
-            nc.vector.reciprocal(out=rstd[:], in_=std_tiles[half][:])
-            result = norm_pool.tile([P, HALF_TILES, D], F32)
-            for i in range(HALF_TILES):
+            scaled_tiles[unit] = scaled
+
+        def finish(unit):
+            scaled, rstd = scaled_tiles[unit], rstd_tiles[unit]
+            b, rows = rows_of(unit)
+            result = norm_pool.tile([P, ROW_TILES, D], F32)
+            for j in range(ROW_TILES):
                 nc.vector.scalar_tensor_tensor(
-                    out=result[:, i, :], in0=scaled[:, i, :], scalar=rstd[:, i : i + 1], in1=beta_all,
+                    out=result[:, j, :], in0=scaled[:, j, :], scalar=rstd[:, j : j + 1], in1=beta_all,
                     op0=ALU.mult, op1=ALU.add,
                 )
-            tiles = slice(half % 2 * HALF_TILES, (half % 2 + 1) * HALF_TILES)
-            nc.sync.dma_start(
-                out=out[b, row0 : row0 + UNIT_ROWS, :].rearrange("(p j) d -> p j d", j=ROW_TILES)[:, tiles, :],
-                in_=result[:],
-            )
+            nc.sync.dma_start(out=out[b, rows, :].rearrange("(p j) d -> p j d", j=ROW_TILES), in_=result[:])
 
-        for i in range(HALVES + 4):
-            if i + PREFETCH < STEPS:
+        def live(unit):
+            return 0 <= unit < UNITS
+
+        for i in range(UNITS + 4):
+            if live(i + PREFETCH):
                 load_attn(i + PREFETCH)
-            if i % H == 0 and i // H < UNITS:
-                load_residual(i // H)
-            if 0 <= i - 1 < STEPS:
-                quantise(i - 1)
-            if 0 <= i - 3 < HALVES:
-                sum_heads(i - 3)
-            if 0 <= i - 4 < HALVES:
-                deviation(i - 4)
-            if i < STEPS:
-                transpose(i)
-            if 0 <= i - 3 < HALVES:
-                back_transpose(i - 3)
-            if 0 <= i - 1 < STEPS:
-                multiply(i - 1)
-            if 0 <= i - 4 < HALVES:
-                normalise(i - 4)
-            if 0 <= i - 3 < HALVES:
-                add_residual(i - 3)
+            if live(i):
+                load_residual(i)
+            if live(i - 1):
+                quantise(i - 1, 1)
+            if live(i - 3):
+                centre(i - 3)
+            if live(i):
+                transpose(i, 0)
+            if live(i - 2):
+                back_transpose(i - 2, 0)
+            if live(i - 3):
+                deviation(i - 3)
+            if live(i - 1):
+                multiply(i - 1, 1)
+            if live(i - 2):
+                add_residual(i - 2, 0)
+            if live(i - 4):
+                finish(i - 4)
+            if live(i):
+                quantise(i, 0)
+                transpose(i, 1)
+            if live(i - 2):
+                back_transpose(i - 2, 1)
+            if i == CONSTANTS_ROUND:
+                spread_constants()
+            if live(i):
+                multiply(i, 0)
+            if live(i - 1):
+                sum_heads(i - 1)
+            if live(i - 2):
+                add_residual(i - 2, 1)

@@ -35,7 +35,7 @@ def tile_multiheadattentionunit_pa_t_e_kernel(
     with ExitStack() as stack:
         consts = stack.enter_context(tc.tile_pool(name="consts", bufs=1))
         attn_pool = stack.enter_context(tc.tile_pool(name="attn_pool", bufs=H * (PREFETCH + 1)))
-        resid_pool = stack.enter_context(tc.tile_pool(name="resid_pool", bufs=4))
+        resid_pool = stack.enter_context(tc.tile_pool(name="resid_pool", bufs=6))
         head_pool = stack.enter_context(tc.tile_pool(name="head_pool", bufs=4))
         norm_pool = stack.enter_context(tc.tile_pool(name="norm_pool", bufs=3))
         fwd_psum = stack.enter_context(tc.psum_pool(name="fwd_psum", bufs=4))
@@ -129,7 +129,9 @@ def tile_multiheadattentionunit_pa_t_e_kernel(
                         nc.tensor.transpose(
                             flipped[:, g, u, :], words[:, first : (g + 1) * K_PASS // 2 : PAIRS], ident[:]
                         )
-                nc.scalar.copy(
+                by_vector = unit % 2 == 1 and h == 0 and j == 1
+                copy_out = nc.vector.tensor_copy if by_vector else nc.scalar.copy
+                copy_out(
                     out=grouped_words[:, :, j * P : (j + 1) * P, :],
                     in_=flipped[:].rearrange("p g u r -> p g r u"),
                 )
@@ -248,37 +250,37 @@ def tile_multiheadattentionunit_pa_t_e_kernel(
         def live(unit):
             return 0 <= unit < UNITS
 
-        for i in range(UNITS + 4):
+        for i in range(UNITS + 6):
             if live(i + PREFETCH):
                 load_attn(i + PREFETCH)
             if live(i):
                 load_residual(i)
+            if live(i - 4):
+                add_residual(i - 4, 1)
+            if live(i - 5):
+                finish(i - 5)
             if live(i - 1):
                 quantise(i - 1, 1)
-            if live(i - 3):
-                centre(i - 3)
             if live(i):
                 transpose(i, 0)
-            if live(i - 2):
-                back_transpose(i - 2, 0)
             if live(i - 3):
-                deviation(i - 3)
-            if live(i - 1):
-                multiply(i - 1, 1)
-            if live(i - 2):
-                add_residual(i - 2, 0)
+                back_transpose(i - 3, 0)
             if live(i - 4):
-                finish(i - 4)
-            if live(i):
-                quantise(i, 0)
-                transpose(i, 1)
+                deviation(i - 4)
+            if live(i - 1):
+                multiply(i - 1, 0)
             if live(i - 2):
-                back_transpose(i - 2, 1)
+                sum_heads(i - 2)
+            if live(i - 4):
+                centre(i - 4)
+            if live(i):
+                transpose(i, 1)
+                quantise(i, 0)
+            if live(i - 3):
+                back_transpose(i - 3, 1)
             if i == CONSTANTS_ROUND:
                 spread_constants()
-            if live(i):
-                multiply(i, 0)
             if live(i - 1):
-                sum_heads(i - 1)
-            if live(i - 2):
-                add_residual(i - 2, 1)
+                multiply(i - 1, 1)
+            if live(i - 3):
+                add_residual(i - 3, 0)

@@ -88,8 +88,6 @@ def tile_multiheadattentionunit_pa_t_e_kernel(
         make_identity(nc, ident[:])
         ones = consts.tile([P, P], BF16)
         nc.vector.memset(ones[:], 1.0)
-        neg_half = consts.tile([P, ROW_TILES], F32)
-        nc.vector.memset(neg_half[:], -0.5)
 
         affine_rows = consts.tile([P, 2 * D], BF16)
         nc.vector.memset(affine_rows[:], 0.0)
@@ -198,15 +196,12 @@ def tile_multiheadattentionunit_pa_t_e_kernel(
                 op1=ALU.add,
                 accum_out=rowsum_tiles[unit][:, j : j + 1],
             )
-            if j == ROW_TILES - 1:
-                negmean = norm_pool.tile([P, ROW_TILES], F32)
-                nc.gpsimd.tensor_scalar(
-                    out=negmean[:], in0=rowsum_tiles[unit][:], scalar1=-1.0 / D, scalar2=0.0, op0=ALU.mult, op1=ALU.add
-                )
-                negmean_tiles[unit] = negmean
 
         def deviation(unit):
-            x, negmean = x_tiles[unit], negmean_tiles[unit]
+            x = x_tiles[unit]
+            negmean = norm_pool.tile([P, ROW_TILES], F32)
+            nc.scalar.activation(out=negmean[:], in_=rowsum_tiles[unit][:], func=ACT.Copy, scale=-1.0 / D)
+            negmean_tiles[unit] = negmean
             squares = norm_pool.tile([P, ROW_TILES, D], F32)
             sumsq = norm_pool.tile([P, ROW_TILES], F32)
             for j in range(ROW_TILES):
@@ -218,12 +213,10 @@ def tile_multiheadattentionunit_pa_t_e_kernel(
                     scale=1.0,
                     accum_out=sumsq[:, j : j + 1],
                 )
-            var_eps = norm_pool.tile([P, ROW_TILES], F32)
-            nc.gpsimd.tensor_scalar(
-                out=var_eps[:], in0=sumsq[:], scalar1=1.0 / D, scalar2=LN_EPS, op0=ALU.mult, op1=ALU.add
-            )
             rstd = norm_pool.tile([P, ROW_TILES], F32)
-            nc.gpsimd.tensor_tensor(out=rstd[:], in0=var_eps[:], in1=neg_half[:], op=ALU.pow)
+            nc.scalar.activation(
+                out=rstd[:], in_=sumsq[:], func=ACT.Abs_reciprocal_sqrt, bias=LN_EPS, scale=1.0 / D
+            )
             rstd_tiles[unit] = rstd
 
         def centre(unit):

@@ -37,6 +37,7 @@ def tile_multiheadattentionunit_pa_t_e_kernel(
         attn_pool = stack.enter_context(tc.tile_pool(name="attn_pool", bufs=H * (PREFETCH + 1)))
         resid_pool = stack.enter_context(tc.tile_pool(name="resid_pool", bufs=6))
         head_pool = stack.enter_context(tc.tile_pool(name="head_pool", bufs=4))
+        relu_pool = stack.enter_context(tc.tile_pool(name="relu_pool", bufs=6))
         norm_pool = stack.enter_context(tc.tile_pool(name="norm_pool", bufs=3))
         fwd_psum = stack.enter_context(tc.psum_pool(name="fwd_psum", bufs=4))
         acc_psum = stack.enter_context(tc.psum_pool(name="acc_psum", bufs=2))
@@ -44,7 +45,7 @@ def tile_multiheadattentionunit_pa_t_e_kernel(
         stack.enter_context(tc.manual_schedule())
 
         attn_tiles, grouped_tiles, code_tiles, scale_tiles, relu_tiles = {}, {}, {}, {}, {}
-        resid_tiles, sum_tiles, back_tiles, x_tiles, rowsum_tiles = {}, {}, {}, {}, {}
+        resid_tiles, back_tiles, x_tiles, rowsum_tiles = {}, {}, {}, {}
         negmean_tiles, rstd_tiles, scaled_tiles = {}, {}, {}
 
         def rows_of(unit):
@@ -127,7 +128,7 @@ def tile_multiheadattentionunit_pa_t_e_kernel(
                         nc.tensor.transpose(
                             flipped[:, g, u, :], words[:, first : (g + 1) * K_PASS // 2 : PAIRS], ident[:]
                         )
-                by_vector = unit % 2 == 1 and h == 0 and j == 1
+                by_vector = h == 1 and j == 1
                 copy_out = nc.vector.tensor_copy if by_vector else nc.scalar.copy
                 copy_out(
                     out=grouped_words[:, :, j * P : (j + 1) * P, :],
@@ -147,7 +148,7 @@ def tile_multiheadattentionunit_pa_t_e_kernel(
 
         def multiply(unit, h):
             codes, scales = code_tiles[unit, h], scale_tiles[unit, h]
-            relu = head_pool.tile([P, D_HALVES, UNIT_ROWS], F32)
+            relu = relu_pool.tile([P, D_HALVES, UNIT_ROWS], F32)
             acc = acc_psum.tile([P, D_HALVES, UNIT_ROWS], F32)
             for c in range(D_HALVES):
                 for g in range(PASSES):
@@ -168,19 +169,20 @@ def tile_multiheadattentionunit_pa_t_e_kernel(
                 )
             relu_tiles[unit, h] = relu
 
-        def sum_heads(unit):
-            heads = norm_pool.tile([P, D_HALVES, UNIT_ROWS], F32)
-            nc.vector.tensor_add(out=heads[:], in0=relu_tiles[unit, 0][:], in1=relu_tiles[unit, 1][:])
-            sum_tiles[unit] = heads
-
-        def back_transpose(unit, j):
-            if j == 0:
-                back = back_psum.tile([P, ROW_TILES, D], F32)
-                back_tiles[unit] = back
-            for c in range(D_HALVES):
-                nc.tensor.transpose(
-                    back_tiles[unit][:, j, c * P : (c + 1) * P], sum_tiles[unit][:, c, j * P : (j + 1) * P], ident[:]
-                )
+        def back_transpose(unit):
+            back = back_psum.tile([P, ROW_TILES, D], F32)
+            for j in range(ROW_TILES):
+                for c in range(D_HALVES):
+                    for h in range(H):
+                        nc.tensor.matmul(
+                            out=back[:, j, c * P : (c + 1) * P],
+                            lhsT=relu_tiles[unit, h][:, c, j * P : (j + 1) * P],
+                            rhs=ident[:],
+                            is_transpose=True,
+                            start=(h == 0),
+                            stop=(h == H - 1),
+                        )
+            back_tiles[unit] = back
 
         def add_residual(unit, j):
             if j == 0:
@@ -243,37 +245,33 @@ def tile_multiheadattentionunit_pa_t_e_kernel(
         def live(unit):
             return 0 <= unit < UNITS
 
-        for i in range(UNITS + 6):
+        for i in range(UNITS + 5):
             if live(i + PREFETCH):
                 load_attn(i + PREFETCH)
             if live(i):
                 load_residual(i)
+            if live(i - 3):
+                add_residual(i - 3, 0)
+                add_residual(i - 3, 1)
             if live(i - 4):
-                add_residual(i - 4, 1)
-            if live(i - 5):
-                finish(i - 5)
-            if live(i - 1):
-                quantise(i - 1, 1)
+                finish(i - 4)
             if live(i):
                 transpose(i, 0)
+            if live(i - 1):
+                quantise(i - 1, 1)
             if live(i - 3):
-                back_transpose(i - 3, 0)
-            if live(i - 4):
-                deviation(i - 4)
+                deviation(i - 3)
             if live(i - 1):
                 multiply(i - 1, 0)
-            if live(i - 2):
-                sum_heads(i - 2)
-            if live(i - 4):
-                centre(i - 4)
             if live(i):
-                transpose(i, 1)
                 quantise(i, 0)
             if live(i - 3):
-                back_transpose(i - 3, 1)
+                centre(i - 3)
+            if live(i):
+                transpose(i, 1)
+            if live(i - 2):
+                back_transpose(i - 2)
             if i == CONSTANTS_ROUND:
                 spread_constants()
             if live(i - 1):
                 multiply(i - 1, 1)
-            if live(i - 3):
-                add_residual(i - 3, 0)

@@ -245,33 +245,32 @@ def tile_multiheadattentionunit_pa_t_e_kernel(
         def live(unit):
             return 0 <= unit < UNITS
 
-        for i in range(UNITS + 5):
+        for i in range(UNITS + 6):
             if live(i + PREFETCH):
                 load_attn(i + PREFETCH)
             if live(i):
                 load_residual(i)
-            if live(i - 3):
-                add_residual(i - 3, 0)
-                add_residual(i - 3, 1)
-            if live(i - 4):
-                finish(i - 4)
+            if live(i - 1):
+                quantise(i - 1, 0)
+                quantise(i - 1, 1)
             if live(i):
                 transpose(i, 0)
-            if live(i - 1):
-                quantise(i - 1, 1)
-            if live(i - 3):
-                deviation(i - 3)
-            if live(i - 1):
-                multiply(i - 1, 0)
-            if live(i):
-                quantise(i, 0)
-            if live(i - 3):
-                centre(i - 3)
+            if live(i - 2):
+                multiply(i - 2, 0)
+            if live(i - 4):
+                add_residual(i - 4, 0)
+                add_residual(i - 4, 1)
+            if live(i - 5):
+                centre(i - 5)
             if live(i):
                 transpose(i, 1)
+            if live(i - 5):
+                finish(i - 5)
             if live(i - 2):
-                back_transpose(i - 2)
+                multiply(i - 2, 1)
+            if live(i - 3):
+                back_transpose(i - 3)
             if i == CONSTANTS_ROUND:
                 spread_constants()
-            if live(i - 1):
-                multiply(i - 1, 1)
+            if live(i - 4):
+                deviation(i - 4)

@@ -39,9 +39,7 @@ def tile_multiheadattentionunit_pa_t_e_kernel(
         head_pool = stack.enter_context(tc.tile_pool(name="head_pool", bufs=4))
         relu_pool = stack.enter_context(tc.tile_pool(name="relu_pool", bufs=6))
         norm_pool = stack.enter_context(tc.tile_pool(name="norm_pool", bufs=3))
-        fwd_psum = stack.enter_context(tc.psum_pool(name="fwd_psum", bufs=4))
-        acc_psum = stack.enter_context(tc.psum_pool(name="acc_psum", bufs=2))
-        back_psum = stack.enter_context(tc.psum_pool(name="back_psum", bufs=2))
+        psum = stack.enter_context(tc.psum_pool(name="psum", bufs=8))
         stack.enter_context(tc.manual_schedule())
 
         attn_tiles, grouped_tiles, code_tiles, scale_tiles, relu_tiles = {}, {}, {}, {}, {}
@@ -105,13 +103,13 @@ def tile_multiheadattentionunit_pa_t_e_kernel(
         bias_cols = consts.tile([P, H * D_HALVES], F32)
 
         def spread_constants():
-            spread = acc_psum.tile([P, D_HALVES, UNIT_ROWS], F32, tag="acc")
+            spread = psum.tile([P, D_HALVES, UNIT_ROWS], F32, tag="bank")
             nc.tensor.matmul(
                 out=spread[:].rearrange("p c r -> p (c r)"), lhsT=ones[:], rhs=affine_rows[:], start=True, stop=True
             )
             nc.vector.tensor_copy(out=affine[:], in_=spread[:].rearrange("p c r -> p (c r)"))
             nc.vector.tensor_copy(out=bias_rows_f32[:], in_=bias_rows[:])
-            bias_psum = back_psum.tile([P, ROW_TILES, D], F32, tag="back")
+            bias_psum = psum.tile([P, ROW_TILES, D], F32, tag="bank")
             nc.tensor.transpose(bias_psum[:, 0, 0:P], bias_rows_f32[:], ident[:])
             nc.vector.tensor_copy(out=bias_cols[:], in_=bias_psum[:, 0, 0 : H * D_HALVES])
 
@@ -121,7 +119,7 @@ def tile_multiheadattentionunit_pa_t_e_kernel(
             grouped_words = grouped[:].bitcast(F32)
             for j in range(ROW_TILES):
                 words = x_rows[:, j, :].bitcast(F32)
-                flipped = fwd_psum.tile([P, PASSES, PAIRS, P], F32)
+                flipped = psum.tile([P, PASSES, PAIRS, P], F32, tag="bank")
                 for g in range(PASSES):
                     for u in range(PAIRS):
                         first = g * K_PASS // 2 + u
@@ -149,7 +147,7 @@ def tile_multiheadattentionunit_pa_t_e_kernel(
         def multiply(unit, h):
             codes, scales = code_tiles[unit, h], scale_tiles[unit, h]
             relu = relu_pool.tile([P, D_HALVES, UNIT_ROWS], F32)
-            acc = acc_psum.tile([P, D_HALVES, UNIT_ROWS], F32)
+            acc = psum.tile([P, D_HALVES, UNIT_ROWS], F32, tag="bank")
             for c in range(D_HALVES):
                 for g in range(PASSES):
                     nc.tensor.matmul_mx(
@@ -170,7 +168,7 @@ def tile_multiheadattentionunit_pa_t_e_kernel(
             relu_tiles[unit, h] = relu
 
         def back_transpose(unit):
-            back = back_psum.tile([P, ROW_TILES, D], F32)
+            back = psum.tile([P, ROW_TILES, D], F32, tag="bank")
             for j in range(ROW_TILES):
                 for c in range(D_HALVES):
                     for h in range(H):

@@ -25,6 +25,7 @@ UNIT_ROWS = P * ROW_TILES
 UNITS = B * S // UNIT_ROWS
 D_HALVES = D // P
 PREFETCH = 6
+UNITS_SUMMED_ON_VECTOR = 10
 CONSTANTS_ROUND = 0
 
 
@@ -35,15 +36,15 @@ def tile_multiheadattentionunit_pa_t_e_kernel(
     with ExitStack() as stack:
         consts = stack.enter_context(tc.tile_pool(name="consts", bufs=1))
         attn_pool = stack.enter_context(tc.tile_pool(name="attn_pool", bufs=H * (PREFETCH + 1)))
-        resid_pool = stack.enter_context(tc.tile_pool(name="resid_pool", bufs=6))
+        resid_pool = stack.enter_context(tc.tile_pool(name="resid_pool", bufs=7))
         head_pool = stack.enter_context(tc.tile_pool(name="head_pool", bufs=4))
-        relu_pool = stack.enter_context(tc.tile_pool(name="relu_pool", bufs=6))
+        relu_pool = stack.enter_context(tc.tile_pool(name="relu_pool", bufs=8))
         norm_pool = stack.enter_context(tc.tile_pool(name="norm_pool", bufs=3))
         psum = stack.enter_context(tc.psum_pool(name="psum", bufs=8))
         stack.enter_context(tc.manual_schedule())
 
         attn_tiles, grouped_tiles, code_tiles, scale_tiles, relu_tiles = {}, {}, {}, {}, {}
-        resid_tiles, back_tiles, x_tiles, rowsum_tiles = {}, {}, {}, {}
+        resid_tiles, sum_tiles, back_tiles, x_tiles, rowsum_tiles = {}, {}, {}, {}, {}
         negmean_tiles, rstd_tiles, scaled_tiles = {}, {}, {}
 
         def rows_of(unit):
@@ -53,9 +54,14 @@ def tile_multiheadattentionunit_pa_t_e_kernel(
             b, rows = rows_of(unit)
             for h in range(H):
                 x_rows = attn_pool.tile([P, ROW_TILES, DV], BF16)
-                nc.sync.dma_start(
-                    out=x_rows[:], in_=attn[b, h, rows, :].rearrange("(p j) k -> p j k", j=ROW_TILES)
-                )
+                source = attn[b, h, rows, :].rearrange("(p j) k -> p j k", j=ROW_TILES)
+                if unit == 0:
+                    for j in range(ROW_TILES):
+                        for g in range(PASSES):
+                            piece = slice(g * K_PASS, (g + 1) * K_PASS)
+                            nc.sync.dma_start(out=x_rows[:, j, piece], in_=source[:, j, piece])
+                else:
+                    nc.sync.dma_start(out=x_rows[:], in_=source)
                 attn_tiles[unit, h] = x_rows
 
         def load_residual(unit):
@@ -167,18 +173,24 @@ def tile_multiheadattentionunit_pa_t_e_kernel(
                 )
             relu_tiles[unit, h] = relu
 
+        def sum_heads(unit):
+            heads = norm_pool.tile([P, D_HALVES, UNIT_ROWS], F32)
+            nc.vector.tensor_add(out=heads[:], in0=relu_tiles[unit, 0][:], in1=relu_tiles[unit, 1][:])
+            sum_tiles[unit] = heads
+
         def back_transpose(unit):
             back = psum.tile([P, ROW_TILES, D], F32, tag="bank")
             for j in range(ROW_TILES):
                 for c in range(D_HALVES):
-                    for h in range(H):
+                    terms = [sum_tiles[unit]] if unit < UNITS_SUMMED_ON_VECTOR else [relu_tiles[unit, h] for h in range(H)]
+                    for n, term in enumerate(terms):
                         nc.tensor.matmul(
                             out=back[:, j, c * P : (c + 1) * P],
-                            lhsT=relu_tiles[unit, h][:, c, j * P : (j + 1) * P],
+                            lhsT=term[:, c, j * P : (j + 1) * P],
                             rhs=ident[:],
                             is_transpose=True,
-                            start=(h == 0),
-                            stop=(h == H - 1),
+                            start=(n == 0),
+                            stop=(n == len(terms) - 1),
                         )
             back_tiles[unit] = back
 
@@ -243,7 +255,7 @@ def tile_multiheadattentionunit_pa_t_e_kernel(
         def live(unit):
             return 0 <= unit < UNITS
 
-        for i in range(UNITS + 6):
+        for i in range(UNITS + 7):
             if live(i + PREFETCH):
                 load_attn(i + PREFETCH)
             if live(i):
@@ -255,20 +267,22 @@ def tile_multiheadattentionunit_pa_t_e_kernel(
                 transpose(i, 0)
             if live(i - 2):
                 multiply(i - 2, 0)
-            if live(i - 4):
-                add_residual(i - 4, 0)
-                add_residual(i - 4, 1)
+            if live(i - 3) and i - 3 < UNITS_SUMMED_ON_VECTOR:
+                sum_heads(i - 3)
             if live(i - 5):
-                centre(i - 5)
+                add_residual(i - 5, 0)
+                add_residual(i - 5, 1)
+            if live(i - 6):
+                centre(i - 6)
             if live(i):
                 transpose(i, 1)
-            if live(i - 5):
-                finish(i - 5)
+            if live(i - 6):
+                finish(i - 6)
             if live(i - 2):
                 multiply(i - 2, 1)
-            if live(i - 3):
-                back_transpose(i - 3)
+            if live(i - 4):
+                back_transpose(i - 4)
             if i == CONSTANTS_ROUND:
                 spread_constants()
-            if live(i - 4):
-                deviation(i - 4)
+            if live(i - 5):
+                deviation(i - 5)

@@ -89,6 +89,10 @@ def tile_multiheadattentionunit_pa_t_e_kernel(
         for unit in range(1, PREFETCH):
             load_attn(unit)
 
+        table_warmer = consts.tile([P, 1], F32)
+        nc.vector.memset(table_warmer[:], 1.0)
+        nc.scalar.activation(out=table_warmer[:], in_=table_warmer[:], func=ACT.Abs_reciprocal_sqrt)
+
         ident = consts.tile([P, P], F32)
         make_identity(nc, ident[:])
         ones = consts.tile([P, P], BF16)
@@ -255,7 +259,7 @@ def tile_multiheadattentionunit_pa_t_e_kernel(
         def live(unit):
             return 0 <= unit < UNITS
 
-        for i in range(UNITS + 7):
+        for i in range(UNITS + 6):
             if live(i + PREFETCH):
                 load_attn(i + PREFETCH)
             if live(i):
@@ -263,26 +267,26 @@ def tile_multiheadattentionunit_pa_t_e_kernel(
             if live(i - 1):
                 quantise(i - 1, 0)
                 quantise(i - 1, 1)
+            if live(i - 3) and i - 3 < UNITS_SUMMED_ON_VECTOR:
+                sum_heads(i - 3)
             if live(i):
                 transpose(i, 0)
             if live(i - 2):
                 multiply(i - 2, 0)
-            if live(i - 3) and i - 3 < UNITS_SUMMED_ON_VECTOR:
-                sum_heads(i - 3)
+            if live(i - 4):
+                add_residual(i - 4, 0)
+                add_residual(i - 4, 1)
             if live(i - 5):
-                add_residual(i - 5, 0)
-                add_residual(i - 5, 1)
-            if live(i - 6):
-                centre(i - 6)
+                centre(i - 5)
             if live(i):
                 transpose(i, 1)
-            if live(i - 6):
-                finish(i - 6)
+            if live(i - 5):
+                finish(i - 5)
             if live(i - 2):
                 multiply(i - 2, 1)
-            if live(i - 4):
-                back_transpose(i - 4)
+            if live(i - 3):
+                back_transpose(i - 3)
             if i == CONSTANTS_ROUND:
                 spread_constants()
-            if live(i - 5):
-                deviation(i - 5)
+            if live(i - 4):
+                deviation(i - 4)

@@ -25,8 +25,8 @@ UNIT_ROWS = P * ROW_TILES
 UNITS = B * S // UNIT_ROWS
 D_HALVES = D // P
 PREFETCH = 6
-UNITS_SUMMED_ON_VECTOR = 10
-CONSTANTS_ROUND = 0
+RESID_LAG = 3
+CONSTANTS_STEP = 1
 
 
 def tile_multiheadattentionunit_pa_t_e_kernel(
@@ -36,14 +36,14 @@ def tile_multiheadattentionunit_pa_t_e_kernel(
     with ExitStack() as stack:
         consts = stack.enter_context(tc.tile_pool(name="consts", bufs=1))
         attn_pool = stack.enter_context(tc.tile_pool(name="attn_pool", bufs=H * (PREFETCH + 1)))
-        resid_pool = stack.enter_context(tc.tile_pool(name="resid_pool", bufs=7))
+        resid_pool = stack.enter_context(tc.tile_pool(name="resid_pool", bufs=8))
         head_pool = stack.enter_context(tc.tile_pool(name="head_pool", bufs=4))
         relu_pool = stack.enter_context(tc.tile_pool(name="relu_pool", bufs=8))
-        norm_pool = stack.enter_context(tc.tile_pool(name="norm_pool", bufs=3))
+        norm_pool = stack.enter_context(tc.tile_pool(name="norm_pool", bufs=4))
         psum = stack.enter_context(tc.psum_pool(name="psum", bufs=8))
         stack.enter_context(tc.manual_schedule())
 
-        attn_tiles, grouped_tiles, code_tiles, scale_tiles, relu_tiles = {}, {}, {}, {}, {}
+        attn_tiles, grouped_tiles, code_tiles, scale_tiles, acc_tiles, first_tiles = {}, {}, {}, {}, {}, {}
         resid_tiles, sum_tiles, back_tiles, x_tiles, rowsum_tiles = {}, {}, {}, {}, {}
         negmean_tiles, rstd_tiles, scaled_tiles = {}, {}, {}
 
@@ -88,6 +88,8 @@ def tile_multiheadattentionunit_pa_t_e_kernel(
             )
         for unit in range(1, PREFETCH):
             load_attn(unit)
+            if unit >= RESID_LAG:
+                load_residual(unit - RESID_LAG)
 
         table_warmer = consts.tile([P, 1], F32)
         nc.vector.memset(table_warmer[:], 1.0)
@@ -95,6 +97,8 @@ def tile_multiheadattentionunit_pa_t_e_kernel(
 
         ident = consts.tile([P, P], F32)
         make_identity(nc, ident[:])
+        ident_bf16 = consts.tile([P, P], BF16)
+        make_identity(nc, ident_bf16[:])
         ones = consts.tile([P, P], BF16)
         nc.vector.memset(ones[:], 1.0)
 
@@ -110,7 +114,10 @@ def tile_multiheadattentionunit_pa_t_e_kernel(
         affine = consts.tile([P, 2 * D], F32)
         gamma_all, beta_all = affine[:, 0:D], affine[:, D : 2 * D]
         bias_rows_f32 = consts.tile([P, P], F32)
-        bias_cols = consts.tile([P, H * D_HALVES], F32)
+        neg_bias = consts.tile([P, H * D_HALVES], F32)
+        bias_sum = consts.tile([P, D_HALVES], F32)
+
+        nc.vector.tensor_copy(out=bias_rows_f32[:], in_=bias_rows[:])
 
         def spread_constants():
             spread = psum.tile([P, D_HALVES, UNIT_ROWS], F32, tag="bank")
@@ -118,10 +125,13 @@ def tile_multiheadattentionunit_pa_t_e_kernel(
                 out=spread[:].rearrange("p c r -> p (c r)"), lhsT=ones[:], rhs=affine_rows[:], start=True, stop=True
             )
             nc.vector.tensor_copy(out=affine[:], in_=spread[:].rearrange("p c r -> p (c r)"))
-            nc.vector.tensor_copy(out=bias_rows_f32[:], in_=bias_rows[:])
             bias_psum = psum.tile([P, ROW_TILES, D], F32, tag="bank")
             nc.tensor.transpose(bias_psum[:, 0, 0:P], bias_rows_f32[:], ident[:])
-            nc.vector.tensor_copy(out=bias_cols[:], in_=bias_psum[:, 0, 0 : H * D_HALVES])
+            nc.vector.tensor_scalar_mul(neg_bias[:], bias_psum[:, 0, 0 : H * D_HALVES], -1.0)
+            nc.vector.scalar_tensor_tensor(
+                out=bias_sum[:], in0=neg_bias[:, 0:D_HALVES], scalar=-1.0, in1=neg_bias[:, D_HALVES : 2 * D_HALVES],
+                op0=ALU.mult, op1=ALU.subtract,
+            )
 
         def transpose(unit, h):
             x_rows = attn_tiles[unit, h]
@@ -136,9 +146,7 @@ def tile_multiheadattentionunit_pa_t_e_kernel(
                         nc.tensor.transpose(
                             flipped[:, g, u, :], words[:, first : (g + 1) * K_PASS // 2 : PAIRS], ident[:]
                         )
-                by_vector = h == 1 and j == 1
-                copy_out = nc.vector.tensor_copy if by_vector else nc.scalar.copy
-                copy_out(
+                nc.scalar.copy(
                     out=grouped_words[:, :, j * P : (j + 1) * P, :],
                     in_=flipped[:].rearrange("p g u r -> p g r u"),
                 )
@@ -156,7 +164,6 @@ def tile_multiheadattentionunit_pa_t_e_kernel(
 
         def multiply(unit, h):
             codes, scales = code_tiles[unit, h], scale_tiles[unit, h]
-            relu = relu_pool.tile([P, D_HALVES, UNIT_ROWS], F32)
             acc = psum.tile([P, D_HALVES, UNIT_ROWS], F32, tag="bank")
             for c in range(D_HALVES):
                 for g in range(PASSES):
@@ -169,49 +176,53 @@ def tile_multiheadattentionunit_pa_t_e_kernel(
                         start=(g == 0),
                         stop=(g == PASSES - 1),
                     )
-            for c in range(D_HALVES):
-                column = h * D_HALVES + c
-                nc.scalar.activation(
-                    out=relu[:, c, :], in_=acc[:, c, :], func=ACT.Relu,
-                    bias=bias_cols[:, column : column + 1], scale=1.0,
-                )
-            relu_tiles[unit, h] = relu
+            acc_tiles[unit, h] = acc
 
-        def sum_heads(unit):
-            heads = norm_pool.tile([P, D_HALVES, UNIT_ROWS], F32)
-            nc.vector.tensor_add(out=heads[:], in0=relu_tiles[unit, 0][:], in1=relu_tiles[unit, 1][:])
+        def first_head(unit):
+            first = relu_pool.tile([P, D_HALVES, UNIT_ROWS], F32)
+            for c in range(D_HALVES):
+                nc.vector.tensor_scalar(
+                    out=first[:, c, :], in0=acc_tiles[unit, 0][:, c, :],
+                    scalar1=neg_bias[:, c : c + 1], scalar2=bias_sum[:, c : c + 1],
+                    op0=ALU.max, op1=ALU.add,
+                )
+            first_tiles[unit] = first
+
+        def second_head(unit):
+            heads = relu_pool.tile([P, D_HALVES, UNIT_ROWS], F32)
+            for c in range(D_HALVES):
+                column = D_HALVES + c
+                nc.vector.scalar_tensor_tensor(
+                    out=heads[:, c, :], in0=acc_tiles[unit, 1][:, c, :], scalar=neg_bias[:, column : column + 1],
+                    in1=first_tiles[unit][:, c, :], op0=ALU.max, op1=ALU.add,
+                )
             sum_tiles[unit] = heads
 
         def back_transpose(unit):
             back = psum.tile([P, ROW_TILES, D], F32, tag="bank")
             for j in range(ROW_TILES):
+                nc.tensor.matmul(
+                    out=back[:, j, :], lhsT=ident_bf16[:], rhs=resid_tiles[unit][:, j, :], start=True, stop=False
+                )
                 for c in range(D_HALVES):
-                    terms = [sum_tiles[unit]] if unit < UNITS_SUMMED_ON_VECTOR else [relu_tiles[unit, h] for h in range(H)]
-                    for n, term in enumerate(terms):
-                        nc.tensor.matmul(
-                            out=back[:, j, c * P : (c + 1) * P],
-                            lhsT=term[:, c, j * P : (j + 1) * P],
-                            rhs=ident[:],
-                            is_transpose=True,
-                            start=(n == 0),
-                            stop=(n == len(terms) - 1),
-                        )
+                    nc.tensor.matmul(
+                        out=back[:, j, c * P : (c + 1) * P],
+                        lhsT=sum_tiles[unit][:, c, j * P : (j + 1) * P],
+                        rhs=ident[:],
+                        is_transpose=True,
+                        start=False,
+                        stop=(c == D_HALVES - 1),
+                    )
             back_tiles[unit] = back
 
-        def add_residual(unit, j):
-            if j == 0:
-                x = norm_pool.tile([P, ROW_TILES, D], F32)
-                rowsum = norm_pool.tile([P, ROW_TILES], F32)
-                x_tiles[unit], rowsum_tiles[unit] = x, rowsum
-            nc.vector.scalar_tensor_tensor(
-                out=x_tiles[unit][:, j, :],
-                in0=back_tiles[unit][:, j, :],
-                scalar=1.0,
-                in1=resid_tiles[unit][:, j, :],
-                op0=ALU.mult,
-                op1=ALU.add,
-                accum_out=rowsum_tiles[unit][:, j : j + 1],
-            )
+        def take_out(unit):
+            x = norm_pool.tile([P, ROW_TILES, D], F32)
+            rowsum = norm_pool.tile([P, ROW_TILES], F32)
+            for j in range(ROW_TILES):
+                nc.scalar.activation(
+                    out=x[:, j, :], in_=back_tiles[unit][:, j, :], func=ACT.Copy, accum_out=rowsum[:, j : j + 1]
+                )
+            x_tiles[unit], rowsum_tiles[unit] = x, rowsum
 
         def deviation(unit):
             x = x_tiles[unit]
@@ -259,34 +270,35 @@ def tile_multiheadattentionunit_pa_t_e_kernel(
         def live(unit):
             return 0 <= unit < UNITS
 
-        for i in range(UNITS + 6):
-            if live(i + PREFETCH):
-                load_attn(i + PREFETCH)
+        for step in range(H * (UNITS + 5)):
+            i, h = divmod(step, H)
+            if h == 0:
+                if live(i + PREFETCH):
+                    load_attn(i + PREFETCH)
+                if live(i + PREFETCH - RESID_LAG):
+                    load_residual(i + PREFETCH - RESID_LAG)
+                if live(i - 2):
+                    second_head(i - 2)
+                if live(i - 1):
+                    quantise(i - 1, 1)
+                if live(i - 4):
+                    centre(i - 4)
+            else:
+                if live(i - 1):
+                    first_head(i - 1)
+                if live(i):
+                    quantise(i, 0)
+                if live(i - 4):
+                    finish(i - 4)
             if live(i):
-                load_residual(i)
+                transpose(i, h)
+            if h == 0 and live(i - 3):
+                take_out(i - 3)
+            if h == 1 and live(i - 3):
+                deviation(i - 3)
+            if h == 1 and live(i - 2):
+                back_transpose(i - 2)
             if live(i - 1):
-                quantise(i - 1, 0)
-                quantise(i - 1, 1)
-            if live(i - 3) and i - 3 < UNITS_SUMMED_ON_VECTOR:
-                sum_heads(i - 3)
-            if live(i):
-                transpose(i, 0)
-            if live(i - 2):
-                multiply(i - 2, 0)
-            if live(i - 4):
-                add_residual(i - 4, 0)
-                add_residual(i - 4, 1)
-            if live(i - 5):
-                centre(i - 5)
-            if live(i):
-                transpose(i, 1)
-            if live(i - 5):
-                finish(i - 5)
-            if live(i - 2):
-                multiply(i - 2, 1)
-            if live(i - 3):
-                back_transpose(i - 3)
-            if i == CONSTANTS_ROUND:
+                multiply(i - 1, h)
+            if step == CONSTANTS_STEP:
                 spread_constants()
-            if live(i - 4):
-                deviation(i - 4)

@@ -25,6 +25,8 @@ UNIT_ROWS = P * ROW_TILES
 UNITS = B * S // UNIT_ROWS
 D_HALVES = D // P
 PREFETCH = 6
+EARLY_TILE, LATE_TILE = 1, 0
+SORTED_BLOCKS = ()
 RESID_LAG = 3
 CONSTANTS_STEP = 1
 
@@ -37,15 +39,19 @@ def tile_multiheadattentionunit_pa_t_e_kernel(
         consts = stack.enter_context(tc.tile_pool(name="consts", bufs=1))
         attn_pool = stack.enter_context(tc.tile_pool(name="attn_pool", bufs=H * (PREFETCH + 1)))
         resid_pool = stack.enter_context(tc.tile_pool(name="resid_pool", bufs=8))
+        sort_pool = stack.enter_context(tc.tile_pool(name="sort_pool", bufs=3))
         head_pool = stack.enter_context(tc.tile_pool(name="head_pool", bufs=4))
         relu_pool = stack.enter_context(tc.tile_pool(name="relu_pool", bufs=8))
         norm_pool = stack.enter_context(tc.tile_pool(name="norm_pool", bufs=4))
-        psum = stack.enter_context(tc.psum_pool(name="psum", bufs=8))
+        flip_psum = stack.enter_context(tc.psum_pool(name="flip_psum", bufs=4))
+        acc_psum = stack.enter_context(tc.psum_pool(name="acc_psum", bufs=2))
+        back_psum = stack.enter_context(tc.psum_pool(name="back_psum", bufs=2))
         stack.enter_context(tc.manual_schedule())
 
-        attn_tiles, grouped_tiles, code_tiles, scale_tiles, acc_tiles, first_tiles = {}, {}, {}, {}, {}, {}
-        resid_tiles, sum_tiles, back_tiles, x_tiles, rowsum_tiles = {}, {}, {}, {}, {}
-        negmean_tiles, rstd_tiles, scaled_tiles = {}, {}, {}
+        attn_tiles, sorted_tiles, flipped_tiles, grouped_tiles, code_tiles, scale_tiles = {}, {}, {}, {}, {}, {}
+        acc_tiles, first_tiles = {}, {}
+        resid_tiles, sum_tiles, bank_tiles, back_tiles, unused_tiles = {}, {}, {}, {}, {}
+        negmean_tiles, sumsq_tiles, rstd_tiles, scaled_tiles, square_tiles, result_tiles = {}, {}, {}, {}, {}, {}
 
         def rows_of(unit):
             return unit * UNIT_ROWS // S, slice(unit * UNIT_ROWS % S, unit * UNIT_ROWS % S + UNIT_ROWS)
@@ -68,7 +74,7 @@ def tile_multiheadattentionunit_pa_t_e_kernel(
             b, rows = rows_of(unit)
             resid = resid_pool.tile([P, ROW_TILES, D], BF16)
             nc.sync.dma_start(
-                out=resid[:], in_=query_inputs[b, rows, :].rearrange("(p j) d -> p j d", j=ROW_TILES)
+                out=resid[:], in_=query_inputs[b, rows, :].rearrange("(p j) k -> p j k", j=ROW_TILES)
             )
             resid_tiles[unit] = resid
 
@@ -120,12 +126,12 @@ def tile_multiheadattentionunit_pa_t_e_kernel(
         nc.vector.tensor_copy(out=bias_rows_f32[:], in_=bias_rows[:])
 
         def spread_constants():
-            spread = psum.tile([P, D_HALVES, UNIT_ROWS], F32, tag="bank")
+            spread = acc_psum.tile([P, D_HALVES, UNIT_ROWS], F32, tag="bank")
             nc.tensor.matmul(
                 out=spread[:].rearrange("p c r -> p (c r)"), lhsT=ones[:], rhs=affine_rows[:], start=True, stop=True
             )
             nc.vector.tensor_copy(out=affine[:], in_=spread[:].rearrange("p c r -> p (c r)"))
-            bias_psum = psum.tile([P, ROW_TILES, D], F32, tag="bank")
+            bias_psum = flip_psum.tile([P, ROW_TILES, D], F32, tag="bank")
             nc.tensor.transpose(bias_psum[:, 0, 0:P], bias_rows_f32[:], ident[:])
             nc.vector.tensor_scalar_mul(neg_bias[:], bias_psum[:, 0, 0 : H * D_HALVES], -1.0)
             nc.vector.scalar_tensor_tensor(
@@ -133,38 +139,49 @@ def tile_multiheadattentionunit_pa_t_e_kernel(
                 op0=ALU.mult, op1=ALU.subtract,
             )
 
-        def transpose(unit, h):
-            x_rows = attn_tiles[unit, h]
-            grouped = head_pool.tile([P, PASSES, UNIT_ROWS, 4], BF16, align_bytes=64)
-            grouped_words = grouped[:].bitcast(F32)
-            for j in range(ROW_TILES):
-                words = x_rows[:, j, :].bitcast(F32)
-                flipped = psum.tile([P, PASSES, PAIRS, P], F32, tag="bank")
-                for g in range(PASSES):
-                    for u in range(PAIRS):
-                        first = g * K_PASS // 2 + u
-                        nc.tensor.transpose(
-                            flipped[:, g, u, :], words[:, first : (g + 1) * K_PASS // 2 : PAIRS], ident[:]
-                        )
-                nc.scalar.copy(
-                    out=grouped_words[:, :, j * P : (j + 1) * P, :],
-                    in_=flipped[:].rearrange("p g u r -> p g r u"),
-                )
-            grouped_tiles[unit, h] = grouped
+        def sort_words(unit, h, j):
+            ordered = sort_pool.tile([P, PASSES, PAIRS, P], F32)
+            nc.vector.tensor_copy(
+                out=ordered[:],
+                in_=attn_tiles[unit, h][:, j, :].bitcast(F32).rearrange("p (g m u) -> p g u m", g=PASSES, u=PAIRS),
+            )
+            sorted_tiles[unit, h, j] = ordered
+
+        def flip(unit, h, j):
+            words = attn_tiles[unit, h][:, j, :].bitcast(F32)
+            flipped = flip_psum.tile([P, PASSES, PAIRS, P], F32, tag="bank")
+            for g in range(PASSES):
+                for u in range(PAIRS):
+                    first = g * K_PASS // 2 + u
+                    if (h, j) in SORTED_BLOCKS:
+                        source = sorted_tiles[unit, h, j][:, g, u, :]
+                    else:
+                        source = words[:, first : (g + 1) * K_PASS // 2 : PAIRS]
+                    nc.tensor.transpose(flipped[:, g, u, :], source, ident[:])
+            flipped_tiles[unit, h, j] = flipped
+
+        def copy_out(unit, h, j):
+            if j == 0:
+                grouped = head_pool.tile([P, PASSES, UNIT_ROWS, 4], BF16, align_bytes=64)
+                grouped_tiles[unit, h] = grouped
+            nc.scalar.copy(
+                out=grouped_tiles[unit, h][:].bitcast(F32)[:, :, j * P : (j + 1) * P, :],
+                in_=flipped_tiles[unit, h, j][:].rearrange("p g u r -> p g r u"),
+            )
 
         def quantise(unit, h):
             codes = head_pool.tile([P, PASSES, UNIT_ROWS], U32, align_bytes=64)
             scales = head_pool.tile([P, PASSES, UNIT_ROWS], U8, align_bytes=64)
+            code_tiles[unit, h], scale_tiles[unit, h] = codes, scales
             nc.vector.quantize_mx(
                 out=codes[:].rearrange("p g c -> p (g c)").bitcast(FP8X4),
                 scales=scales[:].rearrange("p g c -> p (g c)"),
                 in_=grouped_tiles[unit, h][:].rearrange("p g c t -> p (g c t)"),
             )
-            code_tiles[unit, h], scale_tiles[unit, h] = codes, scales
 
         def multiply(unit, h):
             codes, scales = code_tiles[unit, h], scale_tiles[unit, h]
-            acc = psum.tile([P, D_HALVES, UNIT_ROWS], F32, tag="bank")
+            acc = acc_psum.tile([P, D_HALVES, UNIT_ROWS], F32, tag="bank")
             for c in range(D_HALVES):
                 for g in range(PASSES):
                     nc.tensor.matmul_mx(
@@ -198,78 +215,82 @@ def tile_multiheadattentionunit_pa_t_e_kernel(
                 )
             sum_tiles[unit] = heads
 
-        def back_transpose(unit):
-            back = psum.tile([P, ROW_TILES, D], F32, tag="bank")
-            for j in range(ROW_TILES):
+        def bring_back(unit, j):
+            if unit not in bank_tiles:
+                bank_tiles[unit] = back_psum.tile([P, ROW_TILES, D], F32, tag="bank", name="back")
+            back = bank_tiles[unit][:, j, :]
+
+            def add_residual(first):
                 nc.tensor.matmul(
-                    out=back[:, j, :], lhsT=ident_bf16[:], rhs=resid_tiles[unit][:, j, :], start=True, stop=False
+                    out=back, lhsT=ident_bf16[:], rhs=resid_tiles[unit][:, j, :], start=first, stop=not first
                 )
+
+            def add_heads(first):
                 for c in range(D_HALVES):
                     nc.tensor.matmul(
-                        out=back[:, j, c * P : (c + 1) * P],
+                        out=back[:, c * P : (c + 1) * P],
                         lhsT=sum_tiles[unit][:, c, j * P : (j + 1) * P],
                         rhs=ident[:],
                         is_transpose=True,
-                        start=False,
-                        stop=(c == D_HALVES - 1),
+                        start=first and c == 0,
+                        stop=not first and c == D_HALVES - 1,
                     )
-            back_tiles[unit] = back
 
-        def take_out(unit):
-            x = norm_pool.tile([P, ROW_TILES, D], F32)
-            rowsum = norm_pool.tile([P, ROW_TILES], F32)
-            for j in range(ROW_TILES):
-                nc.scalar.activation(
-                    out=x[:, j, :], in_=back_tiles[unit][:, j, :], func=ACT.Copy, accum_out=rowsum[:, j : j + 1]
-                )
-            x_tiles[unit], rowsum_tiles[unit] = x, rowsum
+            add_residual(True)
+            add_heads(False)
+            back_tiles[unit, j] = back
 
-        def deviation(unit):
-            x = x_tiles[unit]
-            negmean = norm_pool.tile([P, ROW_TILES], F32)
-            nc.scalar.activation(out=negmean[:], in_=rowsum_tiles[unit][:], func=ACT.Copy, scale=-1.0 / D)
-            negmean_tiles[unit] = negmean
-            squares = norm_pool.tile([P, ROW_TILES, D], F32)
-            sumsq = norm_pool.tile([P, ROW_TILES], F32)
-            for j in range(ROW_TILES):
-                nc.scalar.activation(
-                    out=squares[:, j, :],
-                    in_=x[:, j, :],
-                    func=ACT.Square,
-                    bias=negmean[:, j : j + 1],
-                    scale=1.0,
-                    accum_out=sumsq[:, j : j + 1],
-                )
-            rstd = norm_pool.tile([P, ROW_TILES], F32)
+        def take_mean(unit, j):
+            if unit not in unused_tiles:
+                unused_tiles[unit] = norm_pool.tile([P, ROW_TILES, D], F32, name="unused")
+                negmean_tiles[unit] = norm_pool.tile([P, ROW_TILES], F32, name="negmean")
             nc.scalar.activation(
-                out=rstd[:], in_=sumsq[:], func=ACT.Abs_reciprocal_sqrt, bias=LN_EPS, scale=1.0 / D
+                out=unused_tiles[unit][:, j, :], in_=back_tiles[unit, j], func=ACT.Copy, scale=-1.0 / D,
+                accum_out=negmean_tiles[unit][:, j : j + 1],
             )
-            rstd_tiles[unit] = rstd
 
-        def centre(unit):
-            x, negmean = x_tiles[unit], negmean_tiles[unit]
-            scaled = norm_pool.tile([P, ROW_TILES, D], F32)
-            for j in range(ROW_TILES):
-                nc.vector.scalar_tensor_tensor(
-                    out=scaled[:, j, :], in0=x[:, j, :], scalar=negmean[:, j : j + 1], in1=gamma_all,
-                    op0=ALU.add, op1=ALU.mult,
-                )
-            scaled_tiles[unit] = scaled
+        def squares_of(unit, j):
+            if unit not in square_tiles:
+                square_tiles[unit] = norm_pool.tile([P, ROW_TILES, D], F32, name="squares")
+                sumsq_tiles[unit] = norm_pool.tile([P, ROW_TILES], F32, name="sumsq")
+            nc.scalar.activation(
+                out=square_tiles[unit][:, j, :], in_=back_tiles[unit, j], func=ACT.Square,
+                bias=negmean_tiles[unit][:, j : j + 1], scale=1.0, accum_out=sumsq_tiles[unit][:, j : j + 1],
+            )
 
-        def finish(unit):
-            scaled, rstd = scaled_tiles[unit], rstd_tiles[unit]
+        def inverse_deviation(unit, j, n):
+            if unit not in rstd_tiles:
+                rstd_tiles[unit] = norm_pool.tile([P, ROW_TILES], F32, name="rstd")
+            nc.scalar.activation(
+                out=rstd_tiles[unit][:, j : j + n], in_=sumsq_tiles[unit][:, j : j + n], func=ACT.Abs_reciprocal_sqrt,
+                bias=LN_EPS, scale=1.0 / D,
+            )
+
+        def centre(unit, j):
+            if unit not in scaled_tiles:
+                scaled_tiles[unit] = norm_pool.tile([P, ROW_TILES, D], F32, name="scaled")
+            nc.vector.scalar_tensor_tensor(
+                out=scaled_tiles[unit][:, j, :], in0=back_tiles[unit, j], scalar=negmean_tiles[unit][:, j : j + 1],
+                in1=gamma_all, op0=ALU.add, op1=ALU.mult,
+            )
+
+        def finish(unit, j):
+            if unit not in result_tiles:
+                result_tiles[unit] = norm_pool.tile([P, ROW_TILES, D], F32, name="result")
+            nc.vector.scalar_tensor_tensor(
+                out=result_tiles[unit][:, j, :], in0=scaled_tiles[unit][:, j, :], scalar=rstd_tiles[unit][:, j : j + 1],
+                in1=beta_all, op0=ALU.mult, op1=ALU.add,
+            )
+
+        def store(unit):
             b, rows = rows_of(unit)
-            result = norm_pool.tile([P, ROW_TILES, D], F32)
-            for j in range(ROW_TILES):
-                nc.vector.scalar_tensor_tensor(
-                    out=result[:, j, :], in0=scaled[:, j, :], scalar=rstd[:, j : j + 1], in1=beta_all,
-                    op0=ALU.mult, op1=ALU.add,
-                )
-            nc.sync.dma_start(out=out[b, rows, :].rearrange("(p j) d -> p j d", j=ROW_TILES), in_=result[:])
+            nc.sync.dma_start(out=out[b, rows, :].rearrange("(p j) k -> p j k", j=ROW_TILES), in_=result_tiles[unit][:])
 
         def live(unit):
             return 0 <= unit < UNITS
 
+        for h, j in SORTED_BLOCKS:
+            sort_words(0, h, j)
         for step in range(H * (UNITS + 5)):
             i, h = divmod(step, H)
             if h == 0:
@@ -282,23 +303,39 @@ def tile_multiheadattentionunit_pa_t_e_kernel(
                 if live(i - 1):
                     quantise(i - 1, 1)
                 if live(i - 4):
-                    centre(i - 4)
+                    finish(i - 4, EARLY_TILE)
+                    finish(i - 4, LATE_TILE)
+                    store(i - 4)
+                if live(i - 3):
+                    take_mean(i - 3, EARLY_TILE)
+                    take_mean(i - 3, LATE_TILE)
             else:
                 if live(i - 1):
                     first_head(i - 1)
                 if live(i):
                     quantise(i, 0)
-                if live(i - 4):
-                    finish(i - 4)
+                if live(i - 3):
+                    squares_of(i - 3, EARLY_TILE)
+                    squares_of(i - 3, LATE_TILE)
+                    centre(i - 3, EARLY_TILE)
+                    centre(i - 3, LATE_TILE)
             if live(i):
-                transpose(i, h)
-            if h == 0 and live(i - 3):
-                take_out(i - 3)
+                flip(i, h, 0)
+                copy_out(i, h, 0)
             if h == 1 and live(i - 3):
-                deviation(i - 3)
+                inverse_deviation(i - 3, 0, ROW_TILES)
+            if live(i):
+                flip(i, h, 1)
+                copy_out(i, h, 1)
             if h == 1 and live(i - 2):
-                back_transpose(i - 2)
+                bring_back(i - 2, EARLY_TILE)
+                bring_back(i - 2, LATE_TILE)
             if live(i - 1):
                 multiply(i - 1, h)
             if step == CONSTANTS_STEP:
                 spread_constants()
+            ahead = divmod(step + 2, H)
+            if live(ahead[0]):
+                for j in range(ROW_TILES):
+                    if (ahead[1], j) in SORTED_BLOCKS:
+                        sort_words(ahead[0], ahead[1], j)

@@ -20,14 +20,14 @@ P = 128
 K_PASS = 4 * P
 PASSES = DV // K_PASS
 PAIRS = 2
-ROW_TILES = 2
-UNIT_ROWS = P * ROW_TILES
-UNITS = B * S // UNIT_ROWS
+MOST_TILES = 2
+LARGE_UNITS, SMALL_UNITS = 16, 0
+UNIT_TILES = [MOST_TILES] * LARGE_UNITS + [1] * SMALL_UNITS
+UNITS = len(UNIT_TILES)
 D_HALVES = D // P
+PIECED = 1
 PREFETCH = 6
-EARLY_TILE, LATE_TILE = 1, 0
-SORTED_BLOCKS = ()
-RESID_LAG = 3
+RESID_LAG = 2
 CONSTANTS_STEP = 1
 
 
@@ -48,37 +48,43 @@ def tile_multiheadattentionunit_pa_t_e_kernel(
         back_psum = stack.enter_context(tc.psum_pool(name="back_psum", bufs=2))
         stack.enter_context(tc.manual_schedule())
 
-        attn_tiles, sorted_tiles, flipped_tiles, grouped_tiles, code_tiles, scale_tiles = {}, {}, {}, {}, {}, {}
+        sorted_tiles = {}
+        attn_tiles, flipped_tiles, grouped_tiles, code_tiles, scale_tiles = {}, {}, {}, {}, {}
         acc_tiles, first_tiles = {}, {}
-        resid_tiles, sum_tiles, bank_tiles, back_tiles, unused_tiles = {}, {}, {}, {}, {}
+        resid_tiles, sum_tiles, back_tiles, unused_tiles = {}, {}, {}, {}
         negmean_tiles, sumsq_tiles, rstd_tiles, scaled_tiles, square_tiles, result_tiles = {}, {}, {}, {}, {}, {}
 
         def rows_of(unit):
-            return unit * UNIT_ROWS // S, slice(unit * UNIT_ROWS % S, unit * UNIT_ROWS % S + UNIT_ROWS)
+            first = P * sum(UNIT_TILES[:unit])
+            return first // S, slice(first % S, first % S + P * UNIT_TILES[unit])
 
-        def load_attn(unit):
+        def row_order(unit):
+            return "(j p) k -> p j k" if unit == UNITS - 1 else "(p j) k -> p j k"
+
+        def load_attn(unit, h):
             b, rows = rows_of(unit)
-            for h in range(H):
-                x_rows = attn_pool.tile([P, ROW_TILES, DV], BF16)
-                source = attn[b, h, rows, :].rearrange("(p j) k -> p j k", j=ROW_TILES)
-                if unit == 0:
-                    for j in range(ROW_TILES):
-                        for g in range(PASSES):
-                            piece = slice(g * K_PASS, (g + 1) * K_PASS)
-                            nc.sync.dma_start(out=x_rows[:, j, piece], in_=source[:, j, piece])
-                else:
-                    nc.sync.dma_start(out=x_rows[:], in_=source)
-                attn_tiles[unit, h] = x_rows
+            x_rows = attn_pool.tile([P, UNIT_TILES[unit], DV], BF16)
+            source = attn[b, h, rows, :].rearrange(row_order(unit), j=UNIT_TILES[unit])
+            if unit < PIECED:
+                for j in range(UNIT_TILES[unit]):
+                    for g in range(PASSES if unit == 0 else 1):
+                        piece = slice(g * K_PASS, (g + 1) * K_PASS) if unit == 0 else slice(0, DV)
+                        nc.sync.dma_start(out=x_rows[:, j, piece], in_=source[:, j, piece])
+            else:
+                nc.sync.dma_start(out=x_rows[:], in_=source)
+            attn_tiles[unit, h] = x_rows
 
         def load_residual(unit):
             b, rows = rows_of(unit)
-            resid = resid_pool.tile([P, ROW_TILES, D], BF16)
+            resid = resid_pool.tile([P, UNIT_TILES[unit], D], BF16)
             nc.sync.dma_start(
-                out=resid[:], in_=query_inputs[b, rows, :].rearrange("(p j) k -> p j k", j=ROW_TILES)
+                out=resid[:], in_=query_inputs[b, rows, :].rearrange(row_order(unit), j=UNIT_TILES[unit])
             )
             resid_tiles[unit] = resid
 
-        load_attn(0)
+        load_attn(0, 0)
+        load_attn(0, 1)
+        load_attn(1, 0)
 
         w_words = consts.tile([P, H * PASSES, D], U32, align_bytes=64)
         nc.sync.dma_start(
@@ -93,7 +99,9 @@ def tile_multiheadattentionunit_pa_t_e_kernel(
                 in_=Wo_scales.bitcast(I32)[:, 4 * quadrant : 4 * quadrant + 4, :].rearrange("c r n -> r c n"),
             )
         for unit in range(1, PREFETCH):
-            load_attn(unit)
+            for h in range(H):
+                if (unit, h) not in attn_tiles:
+                    load_attn(unit, h)
             if unit >= RESID_LAG:
                 load_residual(unit - RESID_LAG)
 
@@ -126,22 +134,22 @@ def tile_multiheadattentionunit_pa_t_e_kernel(
         nc.vector.tensor_copy(out=bias_rows_f32[:], in_=bias_rows[:])
 
         def spread_constants():
-            spread = acc_psum.tile([P, D_HALVES, UNIT_ROWS], F32, tag="bank")
+            spread = acc_psum.tile([P, 2 * D], F32, tag="bank")
             nc.tensor.matmul(
-                out=spread[:].rearrange("p c r -> p (c r)"), lhsT=ones[:], rhs=affine_rows[:], start=True, stop=True
+                out=spread[:], lhsT=ones[:], rhs=affine_rows[:], start=True, stop=True
             )
-            nc.vector.tensor_copy(out=affine[:], in_=spread[:].rearrange("p c r -> p (c r)"))
-            bias_psum = flip_psum.tile([P, ROW_TILES, D], F32, tag="bank")
-            nc.tensor.transpose(bias_psum[:, 0, 0:P], bias_rows_f32[:], ident[:])
-            nc.vector.tensor_scalar_mul(neg_bias[:], bias_psum[:, 0, 0 : H * D_HALVES], -1.0)
+            nc.vector.tensor_copy(out=affine[:], in_=spread[:])
+            bias_psum = flip_psum.tile([P, 4 * P], F32, tag="bank")
+            nc.tensor.transpose(bias_psum[:, 0:P], bias_rows_f32[:], ident[:])
+            nc.vector.tensor_scalar_mul(neg_bias[:], bias_psum[:, 0 : H * D_HALVES], -1.0)
             nc.vector.scalar_tensor_tensor(
                 out=bias_sum[:], in0=neg_bias[:, 0:D_HALVES], scalar=-1.0, in1=neg_bias[:, D_HALVES : 2 * D_HALVES],
                 op0=ALU.mult, op1=ALU.subtract,
             )
 
-        def sort_words(unit, h, j):
+        def sort_words(unit, h, j, copy):
             ordered = sort_pool.tile([P, PASSES, PAIRS, P], F32)
-            nc.vector.tensor_copy(
+            copy(
                 out=ordered[:],
                 in_=attn_tiles[unit, h][:, j, :].bitcast(F32).rearrange("p (g m u) -> p g u m", g=PASSES, u=PAIRS),
             )
@@ -153,7 +161,7 @@ def tile_multiheadattentionunit_pa_t_e_kernel(
             for g in range(PASSES):
                 for u in range(PAIRS):
                     first = g * K_PASS // 2 + u
-                    if (h, j) in SORTED_BLOCKS:
+                    if (unit, h, j) in sorted_tiles:
                         source = sorted_tiles[unit, h, j][:, g, u, :]
                     else:
                         source = words[:, first : (g + 1) * K_PASS // 2 : PAIRS]
@@ -162,7 +170,7 @@ def tile_multiheadattentionunit_pa_t_e_kernel(
 
         def copy_out(unit, h, j):
             if j == 0:
-                grouped = head_pool.tile([P, PASSES, UNIT_ROWS, 4], BF16, align_bytes=64)
+                grouped = head_pool.tile([P, PASSES, P * UNIT_TILES[unit], 4], BF16, align_bytes=64)
                 grouped_tiles[unit, h] = grouped
             nc.scalar.copy(
                 out=grouped_tiles[unit, h][:].bitcast(F32)[:, :, j * P : (j + 1) * P, :],
@@ -170,8 +178,8 @@ def tile_multiheadattentionunit_pa_t_e_kernel(
             )
 
         def quantise(unit, h):
-            codes = head_pool.tile([P, PASSES, UNIT_ROWS], U32, align_bytes=64)
-            scales = head_pool.tile([P, PASSES, UNIT_ROWS], U8, align_bytes=64)
+            codes = head_pool.tile([P, PASSES, P * UNIT_TILES[unit]], U32, align_bytes=64)
+            scales = head_pool.tile([P, PASSES, P * UNIT_TILES[unit]], U8, align_bytes=64)
             code_tiles[unit, h], scale_tiles[unit, h] = codes, scales
             nc.vector.quantize_mx(
                 out=codes[:].rearrange("p g c -> p (g c)").bitcast(FP8X4),
@@ -181,7 +189,8 @@ def tile_multiheadattentionunit_pa_t_e_kernel(
 
         def multiply(unit, h):
             codes, scales = code_tiles[unit, h], scale_tiles[unit, h]
-            acc = acc_psum.tile([P, D_HALVES, UNIT_ROWS], F32, tag="bank")
+            pool = flip_psum if (unit, h) == (UNITS - 1, H - 1) else acc_psum
+            acc = pool.tile([P, D_HALVES, P * UNIT_TILES[unit]], F32, tag="bank")
             for c in range(D_HALVES):
                 for g in range(PASSES):
                     nc.tensor.matmul_mx(
@@ -196,7 +205,7 @@ def tile_multiheadattentionunit_pa_t_e_kernel(
             acc_tiles[unit, h] = acc
 
         def first_head(unit):
-            first = relu_pool.tile([P, D_HALVES, UNIT_ROWS], F32)
+            first = relu_pool.tile([P, D_HALVES, P * UNIT_TILES[unit]], F32)
             for c in range(D_HALVES):
                 nc.vector.tensor_scalar(
                     out=first[:, c, :], in0=acc_tiles[unit, 0][:, c, :],
@@ -206,7 +215,7 @@ def tile_multiheadattentionunit_pa_t_e_kernel(
             first_tiles[unit] = first
 
         def second_head(unit):
-            heads = relu_pool.tile([P, D_HALVES, UNIT_ROWS], F32)
+            heads = relu_pool.tile([P, D_HALVES, P * UNIT_TILES[unit]], F32)
             for c in range(D_HALVES):
                 column = D_HALVES + c
                 nc.vector.scalar_tensor_tensor(
@@ -215,52 +224,46 @@ def tile_multiheadattentionunit_pa_t_e_kernel(
                 )
             sum_tiles[unit] = heads
 
-        def bring_back(unit, j):
-            if unit not in bank_tiles:
-                bank_tiles[unit] = back_psum.tile([P, ROW_TILES, D], F32, tag="bank", name="back")
-            back = bank_tiles[unit][:, j, :]
-
-            def add_residual(first):
+        def bring_back(unit):
+            pool = flip_psum if unit == UNITS - 1 else back_psum
+            back = pool.tile([P, UNIT_TILES[unit], D], F32, tag="bank")
+            nc.tensor.matmul(
+                out=back[:].rearrange("p j d -> p (j d)"), lhsT=ident_bf16[:],
+                rhs=resid_tiles[unit][:].rearrange("p j d -> p (j d)"), start=True, stop=False,
+            )
+            blocks = [(j, c) for j in range(UNIT_TILES[unit]) for c in range(D_HALVES)]
+            for j, c in blocks:
                 nc.tensor.matmul(
-                    out=back, lhsT=ident_bf16[:], rhs=resid_tiles[unit][:, j, :], start=first, stop=not first
+                    out=back[:, j, c * P : (c + 1) * P],
+                    lhsT=sum_tiles[unit][:, c, j * P : (j + 1) * P],
+                    rhs=ident[:],
+                    is_transpose=True,
+                    start=False,
+                    stop=(j, c) == blocks[-1],
                 )
-
-            def add_heads(first):
-                for c in range(D_HALVES):
-                    nc.tensor.matmul(
-                        out=back[:, c * P : (c + 1) * P],
-                        lhsT=sum_tiles[unit][:, c, j * P : (j + 1) * P],
-                        rhs=ident[:],
-                        is_transpose=True,
-                        start=first and c == 0,
-                        stop=not first and c == D_HALVES - 1,
-                    )
-
-            add_residual(True)
-            add_heads(False)
-            back_tiles[unit, j] = back
+            back_tiles[unit] = back
 
         def take_mean(unit, j):
             if unit not in unused_tiles:
-                unused_tiles[unit] = norm_pool.tile([P, ROW_TILES, D], F32, name="unused")
-                negmean_tiles[unit] = norm_pool.tile([P, ROW_TILES], F32, name="negmean")
+                unused_tiles[unit] = norm_pool.tile([P, UNIT_TILES[unit], D], F32, name="unused")
+                negmean_tiles[unit] = norm_pool.tile([P, UNIT_TILES[unit]], F32, name="negmean")
             nc.scalar.activation(
-                out=unused_tiles[unit][:, j, :], in_=back_tiles[unit, j], func=ACT.Copy, scale=-1.0 / D,
+                out=unused_tiles[unit][:, j, :], in_=back_tiles[unit][:, j, :], func=ACT.Copy, scale=-1.0 / D,
                 accum_out=negmean_tiles[unit][:, j : j + 1],
             )
 
         def squares_of(unit, j):
             if unit not in square_tiles:
-                square_tiles[unit] = norm_pool.tile([P, ROW_TILES, D], F32, name="squares")
-                sumsq_tiles[unit] = norm_pool.tile([P, ROW_TILES], F32, name="sumsq")
+                square_tiles[unit] = norm_pool.tile([P, UNIT_TILES[unit], D], F32, name="squares")
+                sumsq_tiles[unit] = norm_pool.tile([P, UNIT_TILES[unit]], F32, name="sumsq")
             nc.scalar.activation(
-                out=square_tiles[unit][:, j, :], in_=back_tiles[unit, j], func=ACT.Square,
+                out=square_tiles[unit][:, j, :], in_=back_tiles[unit][:, j, :], func=ACT.Square,
                 bias=negmean_tiles[unit][:, j : j + 1], scale=1.0, accum_out=sumsq_tiles[unit][:, j : j + 1],
             )
 
         def inverse_deviation(unit, j, n):
             if unit not in rstd_tiles:
-                rstd_tiles[unit] = norm_pool.tile([P, ROW_TILES], F32, name="rstd")
+                rstd_tiles[unit] = norm_pool.tile([P, UNIT_TILES[unit]], F32, name="rstd")
             nc.scalar.activation(
                 out=rstd_tiles[unit][:, j : j + n], in_=sumsq_tiles[unit][:, j : j + n], func=ACT.Abs_reciprocal_sqrt,
                 bias=LN_EPS, scale=1.0 / D,
@@ -268,34 +271,37 @@ def tile_multiheadattentionunit_pa_t_e_kernel(
 
         def centre(unit, j):
             if unit not in scaled_tiles:
-                scaled_tiles[unit] = norm_pool.tile([P, ROW_TILES, D], F32, name="scaled")
+                scaled_tiles[unit] = norm_pool.tile([P, UNIT_TILES[unit], D], F32, name="scaled")
             nc.vector.scalar_tensor_tensor(
-                out=scaled_tiles[unit][:, j, :], in0=back_tiles[unit, j], scalar=negmean_tiles[unit][:, j : j + 1],
+                out=scaled_tiles[unit][:, j, :], in0=back_tiles[unit][:, j, :], scalar=negmean_tiles[unit][:, j : j + 1],
                 in1=gamma_all, op0=ALU.add, op1=ALU.mult,
             )
 
         def finish(unit, j):
             if unit not in result_tiles:
-                result_tiles[unit] = norm_pool.tile([P, ROW_TILES, D], F32, name="result")
+                result_tiles[unit] = norm_pool.tile([P, UNIT_TILES[unit], D], F32, name="result")
             nc.vector.scalar_tensor_tensor(
                 out=result_tiles[unit][:, j, :], in0=scaled_tiles[unit][:, j, :], scalar=rstd_tiles[unit][:, j : j + 1],
                 in1=beta_all, op0=ALU.mult, op1=ALU.add,
             )
 
+        def store_tile(unit, j):
+            b, rows = rows_of(unit)
+            nc.sync.dma_start(out=out[b, rows.start + j * P : rows.start + (j + 1) * P, :], in_=result_tiles[unit][:, j, :])
+
         def store(unit):
             b, rows = rows_of(unit)
-            nc.sync.dma_start(out=out[b, rows, :].rearrange("(p j) k -> p j k", j=ROW_TILES), in_=result_tiles[unit][:])
+            nc.sync.dma_start(out=out[b, rows, :].rearrange("(p j) k -> p j k", j=UNIT_TILES[unit]), in_=result_tiles[unit][:])
 
         def live(unit):
             return 0 <= unit < UNITS
 
-        for h, j in SORTED_BLOCKS:
-            sort_words(0, h, j)
-        for step in range(H * (UNITS + 5)):
+        for step in range(H * UNITS):
             i, h = divmod(step, H)
             if h == 0:
                 if live(i + PREFETCH):
-                    load_attn(i + PREFETCH)
+                    load_attn(i + PREFETCH, 0)
+                    load_attn(i + PREFETCH, 1)
                 if live(i + PREFETCH - RESID_LAG):
                     load_residual(i + PREFETCH - RESID_LAG)
                 if live(i - 2):
@@ -303,39 +309,81 @@ def tile_multiheadattentionunit_pa_t_e_kernel(
                 if live(i - 1):
                     quantise(i - 1, 1)
                 if live(i - 4):
-                    finish(i - 4, EARLY_TILE)
-                    finish(i - 4, LATE_TILE)
+                    for j in range(UNIT_TILES[i - 4]):
+                        finish(i - 4, j)
+                if live(i - 4):
                     store(i - 4)
                 if live(i - 3):
-                    take_mean(i - 3, EARLY_TILE)
-                    take_mean(i - 3, LATE_TILE)
+                    for j in range(UNIT_TILES[i - 3]):
+                        take_mean(i - 3, j)
             else:
                 if live(i - 1):
                     first_head(i - 1)
                 if live(i):
                     quantise(i, 0)
                 if live(i - 3):
-                    squares_of(i - 3, EARLY_TILE)
-                    squares_of(i - 3, LATE_TILE)
-                    centre(i - 3, EARLY_TILE)
-                    centre(i - 3, LATE_TILE)
-            if live(i):
-                flip(i, h, 0)
-                copy_out(i, h, 0)
-            if h == 1 and live(i - 3):
-                inverse_deviation(i - 3, 0, ROW_TILES)
-            if live(i):
-                flip(i, h, 1)
-                copy_out(i, h, 1)
+                    for j in range(UNIT_TILES[i - 3]):
+                        squares_of(i - 3, j)
+                if live(i - 3):
+                    for j in range(UNIT_TILES[i - 3]):
+                        centre(i - 3, j)
+            for j in range(MOST_TILES):
+                flip(i, h, j)
+                copy_out(i, h, j)
+                if j == 0 and h == 1 and live(i - 3):
+                    inverse_deviation(i - 3, 0, UNIT_TILES[i - 3])
             if h == 1 and live(i - 2):
-                bring_back(i - 2, EARLY_TILE)
-                bring_back(i - 2, LATE_TILE)
+                bring_back(i - 2)
             if live(i - 1):
                 multiply(i - 1, h)
+            if h == 1 and live(i + 1):
+                if (i + 1) % 2 == 0 and 1 <= i < 12:
+                    sort_words(i + 1, 1, 1, nc.vector.tensor_copy)
+                if (i + 1) % 2 == 1 and 1 <= i < 12:
+                    sort_words(i + 1, 1, 0, nc.scalar.copy)
             if step == CONSTANTS_STEP:
                 spread_constants()
-            ahead = divmod(step + 2, H)
-            if live(ahead[0]):
-                for j in range(ROW_TILES):
-                    if (ahead[1], j) in SORTED_BLOCKS:
-                        sort_words(ahead[0], ahead[1], j)
+
+        last = UNITS - 1
+        tiles = range(MOST_TILES)
+        multiply(last, 0)
+        quantise(last, 1)
+        second_head(last - 1)
+        multiply(last, 1)
+        first_head(last)
+        for j in tiles:
+            take_mean(last - 2, j)
+        for j in tiles:
+            squares_of(last - 2, j)
+        bring_back(last - 1)
+        second_head(last)
+        for j in tiles:
+            finish(last - 3, j)
+        store(last - 3)
+        inverse_deviation(last - 2, 0, MOST_TILES)
+        for j in tiles:
+            take_mean(last - 1, j)
+        bring_back(last)
+        for j in tiles:
+            squares_of(last - 1, j)
+        for j in tiles:
+            centre(last - 2, j)
+        for j in tiles:
+            finish(last - 2, j)
+        store(last - 2)
+        take_mean(last, 0)
+        inverse_deviation(last - 1, 0, MOST_TILES)
+        take_mean(last, 1)
+        for j in tiles:
+            squares_of(last, j)
+        for j in tiles:
+            centre(last - 1, j)
+        for j in tiles:
+            finish(last - 1, j)
+        store(last - 1)
+        for j in tiles:
+            centre(last, j)
+        for j in tiles:
+            inverse_deviation(last, j, 1)
+            finish(last, j)
+            store_tile(last, j)

@@ -91,12 +91,12 @@ def tile_multiheadattentionunit_pa_t_e_kernel(
             out=w_words[:].bitcast(I32),
             in_=Wo_words.rearrange("c p n t -> p c (n t)").bitcast(I32),
         )
-        w_scales = consts.tile([P, H * PASSES, D], U8, align_bytes=64)
-        nc.vector.memset(w_scales[:].rearrange("p c n -> p (c n)").bitcast(I32), 0)
+        w_scales = consts.tile([P, D], U8, align_bytes=64)
+        nc.vector.memset(w_scales[:].bitcast(I32), 0)
         for quadrant in range(4):
             nc.sync.dma_start(
-                out=w_scales[32 * quadrant : 32 * quadrant + 4, :, :].bitcast(I32),
-                in_=Wo_scales.bitcast(I32)[:, 4 * quadrant : 4 * quadrant + 4, :].rearrange("c r n -> r c n"),
+                out=w_scales[32 * quadrant : 32 * quadrant + 16, :].bitcast(I32),
+                in_=Wo_scales.bitcast(I32)[:, 4 * quadrant : 4 * quadrant + 4, :],
             )
         for unit in range(1, PREFETCH):
             for h in range(H):
@@ -196,7 +196,7 @@ def tile_multiheadattentionunit_pa_t_e_kernel(
                     nc.tensor.matmul_mx(
                         out=acc[:, c, :],
                         lhsT=w_words[:, h * PASSES + g, c * P : (c + 1) * P].bitcast(FP8X4),
-                        lhsT_scale=w_scales[:, h * PASSES + g, c * P : (c + 1) * P],
+                        lhsT_scale=w_scales[4 * (h * PASSES + g) :, c * P : (c + 1) * P],
                         rhs=codes[:, g, :].bitcast(FP8X4),
                         rhs_scale=scales[:, g, :],
                         start=(g == 0),

from contextlib import ExitStack

import concourse.mybir as mybir
from concourse.masks import make_identity

F32 = mybir.dt.float32
BF16 = mybir.dt.bfloat16
I32 = mybir.dt.int32
U32 = mybir.dt.uint32
U8 = mybir.dt.uint8
FP8X4 = mybir.dt.float8_e4m3fn_x4
ALU = mybir.AluOpType
ACT = mybir.ActivationFunctionType

B, H, S, DV, D = 4, 2, 1024, 1024, 256
LN_EPS = 1e-3
FLOPS = 2 * B * H * S * DV * D

P = 128
K_PASS = 4 * P
PASSES = DV // K_PASS
PAIRS = 2
MOST_TILES = 2
LARGE_UNITS, SMALL_UNITS = 16, 0
UNIT_TILES = [MOST_TILES] * LARGE_UNITS + [1] * SMALL_UNITS
UNITS = len(UNIT_TILES)
D_HALVES = D // P
PIECED = 1
PREFETCH = 6
RESID_LAG = 2
CONSTANTS_STEP = 1


def tile_multiheadattentionunit_pa_t_e_kernel(
    tc, attn, Wo_words, Wo_scales, bo, query_inputs, gamma, beta, out
):
    nc = tc.nc
    with ExitStack() as stack:
        consts = stack.enter_context(tc.tile_pool(name="consts", bufs=1))
        attn_pool = stack.enter_context(tc.tile_pool(name="attn_pool", bufs=H * (PREFETCH + 1)))
        resid_pool = stack.enter_context(tc.tile_pool(name="resid_pool", bufs=8))
        sort_pool = stack.enter_context(tc.tile_pool(name="sort_pool", bufs=3))
        head_pool = stack.enter_context(tc.tile_pool(name="head_pool", bufs=4))
        relu_pool = stack.enter_context(tc.tile_pool(name="relu_pool", bufs=8))
        norm_pool = stack.enter_context(tc.tile_pool(name="norm_pool", bufs=4))
        flip_psum = stack.enter_context(tc.psum_pool(name="flip_psum", bufs=4))
        acc_psum = stack.enter_context(tc.psum_pool(name="acc_psum", bufs=2))
        back_psum = stack.enter_context(tc.psum_pool(name="back_psum", bufs=2))
        stack.enter_context(tc.manual_schedule())

        sorted_tiles = {}
        attn_tiles, flipped_tiles, grouped_tiles, code_tiles, scale_tiles = {}, {}, {}, {}, {}
        acc_tiles, first_tiles = {}, {}
        resid_tiles, sum_tiles, back_tiles, unused_tiles = {}, {}, {}, {}
        negmean_tiles, sumsq_tiles, rstd_tiles, scaled_tiles, square_tiles, result_tiles = {}, {}, {}, {}, {}, {}

        def rows_of(unit):
            first = P * sum(UNIT_TILES[:unit])
            return first // S, slice(first % S, first % S + P * UNIT_TILES[unit])

        def row_order(unit):
            return "(j p) k -> p j k" if unit == UNITS - 1 else "(p j) k -> p j k"

        def load_attn(unit, h):
            b, rows = rows_of(unit)
            x_rows = attn_pool.tile([P, UNIT_TILES[unit], DV], BF16)
            source = attn[b, h, rows, :].rearrange(row_order(unit), j=UNIT_TILES[unit])
            if unit < PIECED:
                for j in range(UNIT_TILES[unit]):
                    for g in range(PASSES if unit == 0 else 1):
                        piece = slice(g * K_PASS, (g + 1) * K_PASS) if unit == 0 else slice(0, DV)
                        nc.sync.dma_start(out=x_rows[:, j, piece], in_=source[:, j, piece])
            else:
                nc.sync.dma_start(out=x_rows[:], in_=source)
            attn_tiles[unit, h] = x_rows

        def load_residual(unit):
            b, rows = rows_of(unit)
            resid = resid_pool.tile([P, UNIT_TILES[unit], D], BF16)
            nc.sync.dma_start(
                out=resid[:], in_=query_inputs[b, rows, :].rearrange(row_order(unit), j=UNIT_TILES[unit])
            )
            resid_tiles[unit] = resid

        load_attn(0, 0)
        load_attn(0, 1)
        load_attn(1, 0)

        w_words = consts.tile([P, H * PASSES, D], U32, align_bytes=64)
        nc.sync.dma_start(
            out=w_words[:].bitcast(I32),
            in_=Wo_words.rearrange("c p n t -> p c (n t)").bitcast(I32),
        )
        w_scales = consts.tile([P, D], U8, align_bytes=64)
        nc.vector.memset(w_scales[:].bitcast(I32), 0)
        for quadrant in range(4):
            nc.sync.dma_start(
                out=w_scales[32 * quadrant : 32 * quadrant + 16, :].bitcast(I32),
                in_=Wo_scales.bitcast(I32)[:, 4 * quadrant : 4 * quadrant + 4, :],
            )
        for unit in range(1, PREFETCH):
            for h in range(H):
                if (unit, h) not in attn_tiles:
                    load_attn(unit, h)
            if unit >= RESID_LAG:
                load_residual(unit - RESID_LAG)

        table_warmer = consts.tile([P, 1], F32)
        nc.vector.memset(table_warmer[:], 1.0)
        nc.scalar.activation(out=table_warmer[:], in_=table_warmer[:], func=ACT.Abs_reciprocal_sqrt)

        ident = consts.tile([P, P], F32)
        make_identity(nc, ident[:])
        ident_bf16 = consts.tile([P, P], BF16)
        make_identity(nc, ident_bf16[:])
        ones = consts.tile([P, P], BF16)
        nc.vector.memset(ones[:], 1.0)

        affine_rows = consts.tile([P, 2 * D], BF16)
        nc.vector.memset(affine_rows[:], 0.0)
        nc.scalar.dma_start(out=affine_rows[0:1, 0:D], in_=gamma.rearrange("(o d) -> o d", o=1))
        nc.scalar.dma_start(out=affine_rows[0:1, D : 2 * D], in_=beta.rearrange("(o d) -> o d", o=1))
        bias_rows = consts.tile([P, P], BF16)
        nc.vector.memset(bias_rows[:], 0.0)
        nc.scalar.dma_start(
            out=bias_rows[0 : H * D_HALVES, :], in_=bo.rearrange("h (c d) -> (h c) d", c=D_HALVES)
        )
        affine = consts.tile([P, 2 * D], F32)
        gamma_all, beta_all = affine[:, 0:D], affine[:, D : 2 * D]
        bias_rows_f32 = consts.tile([P, P], F32)
        neg_bias = consts.tile([P, H * D_HALVES], F32)
        bias_sum = consts.tile([P, D_HALVES], F32)

        nc.vector.tensor_copy(out=bias_rows_f32[:], in_=bias_rows[:])

        def spread_constants():
            spread = acc_psum.tile([P, 2 * D], F32, tag="bank")
            nc.tensor.matmul(
                out=spread[:], lhsT=ones[:], rhs=affine_rows[:], start=True, stop=True
            )
            nc.vector.tensor_copy(out=affine[:], in_=spread[:])
            bias_psum = flip_psum.tile([P, 4 * P], F32, tag="bank")
            nc.tensor.transpose(bias_psum[:, 0:P], bias_rows_f32[:], ident[:])
            nc.vector.tensor_scalar_mul(neg_bias[:], bias_psum[:, 0 : H * D_HALVES], -1.0)
            nc.vector.scalar_tensor_tensor(
                out=bias_sum[:], in0=neg_bias[:, 0:D_HALVES], scalar=-1.0, in1=neg_bias[:, D_HALVES : 2 * D_HALVES],
                op0=ALU.mult, op1=ALU.subtract,
            )

        def sort_words(unit, h, j, copy):
            ordered = sort_pool.tile([P, PASSES, PAIRS, P], F32)
            copy(
                out=ordered[:],
                in_=attn_tiles[unit, h][:, j, :].bitcast(F32).rearrange("p (g m u) -> p g u m", g=PASSES, u=PAIRS),
            )
            sorted_tiles[unit, h, j] = ordered

        def flip(unit, h, j):
            words = attn_tiles[unit, h][:, j, :].bitcast(F32)
            flipped = flip_psum.tile([P, PASSES, PAIRS, P], F32, tag="bank")
            for g in range(PASSES):
                for u in range(PAIRS):
                    first = g * K_PASS // 2 + u
                    if (unit, h, j) in sorted_tiles:
                        source = sorted_tiles[unit, h, j][:, g, u, :]
                    else:
                        source = words[:, first : (g + 1) * K_PASS // 2 : PAIRS]
                    nc.tensor.transpose(flipped[:, g, u, :], source, ident[:])
            flipped_tiles[unit, h, j] = flipped

        def copy_out(unit, h, j):
            if j == 0:
                grouped = head_pool.tile([P, PASSES, P * UNIT_TILES[unit], 4], BF16, align_bytes=64)
                grouped_tiles[unit, h] = grouped
            nc.scalar.copy(
                out=grouped_tiles[unit, h][:].bitcast(F32)[:, :, j * P : (j + 1) * P, :],
                in_=flipped_tiles[unit, h, j][:].rearrange("p g u r -> p g r u"),
            )

        def quantise(unit, h):
            codes = head_pool.tile([P, PASSES, P * UNIT_TILES[unit]], U32, align_bytes=64)
            scales = head_pool.tile([P, PASSES, P * UNIT_TILES[unit]], U8, align_bytes=64)
            code_tiles[unit, h], scale_tiles[unit, h] = codes, scales
            nc.vector.quantize_mx(
                out=codes[:].rearrange("p g c -> p (g c)").bitcast(FP8X4),
                scales=scales[:].rearrange("p g c -> p (g c)"),
                in_=grouped_tiles[unit, h][:].rearrange("p g c t -> p (g c t)"),
            )

        def multiply(unit, h):
            codes, scales = code_tiles[unit, h], scale_tiles[unit, h]
            pool = flip_psum if (unit, h) == (UNITS - 1, H - 1) else acc_psum
            acc = pool.tile([P, D_HALVES, P * UNIT_TILES[unit]], F32, tag="bank")
            for c in range(D_HALVES):
                for g in range(PASSES):
                    nc.tensor.matmul_mx(
                        out=acc[:, c, :],
                        lhsT=w_words[:, h * PASSES + g, c * P : (c + 1) * P].bitcast(FP8X4),
                        lhsT_scale=w_scales[4 * (h * PASSES + g) :, c * P : (c + 1) * P],
                        rhs=codes[:, g, :].bitcast(FP8X4),
                        rhs_scale=scales[:, g, :],
                        start=(g == 0),
                        stop=(g == PASSES - 1),
                    )
            acc_tiles[unit, h] = acc

        def first_head(unit):
            first = relu_pool.tile([P, D_HALVES, P * UNIT_TILES[unit]], F32)
            for c in range(D_HALVES):
                nc.vector.tensor_scalar(
                    out=first[:, c, :], in0=acc_tiles[unit, 0][:, c, :],
                    scalar1=neg_bias[:, c : c + 1], scalar2=bias_sum[:, c : c + 1],
                    op0=ALU.max, op1=ALU.add,
                )
            first_tiles[unit] = first

        def second_head(unit):
            heads = relu_pool.tile([P, D_HALVES, P * UNIT_TILES[unit]], F32)
            for c in range(D_HALVES):
                column = D_HALVES + c
                nc.vector.scalar_tensor_tensor(
                    out=heads[:, c, :], in0=acc_tiles[unit, 1][:, c, :], scalar=neg_bias[:, column : column + 1],
                    in1=first_tiles[unit][:, c, :], op0=ALU.max, op1=ALU.add,
                )
            sum_tiles[unit] = heads

        def bring_back(unit):
            pool = flip_psum if unit == UNITS - 1 else back_psum
            back = pool.tile([P, UNIT_TILES[unit], D], F32, tag="bank")
            nc.tensor.matmul(
                out=back[:].rearrange("p j d -> p (j d)"), lhsT=ident_bf16[:],
                rhs=resid_tiles[unit][:].rearrange("p j d -> p (j d)"), start=True, stop=False,
            )
            blocks = [(j, c) for j in range(UNIT_TILES[unit]) for c in range(D_HALVES)]
            for j, c in blocks:
                nc.tensor.matmul(
                    out=back[:, j, c * P : (c + 1) * P],
                    lhsT=sum_tiles[unit][:, c, j * P : (j + 1) * P],
                    rhs=ident[:],
                    is_transpose=True,
                    start=False,
                    stop=(j, c) == blocks[-1],
                )
            back_tiles[unit] = back

        def take_mean(unit, j):
            if unit not in unused_tiles:
                unused_tiles[unit] = norm_pool.tile([P, UNIT_TILES[unit], D], F32, name="unused")
                negmean_tiles[unit] = norm_pool.tile([P, UNIT_TILES[unit]], F32, name="negmean")
            nc.scalar.activation(
                out=unused_tiles[unit][:, j, :], in_=back_tiles[unit][:, j, :], func=ACT.Copy, scale=-1.0 / D,
                accum_out=negmean_tiles[unit][:, j : j + 1],
            )

        def squares_of(unit, j):
            if unit not in square_tiles:
                square_tiles[unit] = norm_pool.tile([P, UNIT_TILES[unit], D], F32, name="squares")
                sumsq_tiles[unit] = norm_pool.tile([P, UNIT_TILES[unit]], F32, name="sumsq")
            nc.scalar.activation(
                out=square_tiles[unit][:, j, :], in_=back_tiles[unit][:, j, :], func=ACT.Square,
                bias=negmean_tiles[unit][:, j : j + 1], scale=1.0, accum_out=sumsq_tiles[unit][:, j : j + 1],
            )

        def inverse_deviation(unit, j, n):
            if unit not in rstd_tiles:
                rstd_tiles[unit] = norm_pool.tile([P, UNIT_TILES[unit]], F32, name="rstd")
            nc.scalar.activation(
                out=rstd_tiles[unit][:, j : j + n], in_=sumsq_tiles[unit][:, j : j + n], func=ACT.Abs_reciprocal_sqrt,
                bias=LN_EPS, scale=1.0 / D,
            )

        def centre(unit, j):
            if unit not in scaled_tiles:
                scaled_tiles[unit] = norm_pool.tile([P, UNIT_TILES[unit], D], F32, name="scaled")
            nc.vector.scalar_tensor_tensor(
                out=scaled_tiles[unit][:, j, :], in0=back_tiles[unit][:, j, :], scalar=negmean_tiles[unit][:, j : j + 1],
                in1=gamma_all, op0=ALU.add, op1=ALU.mult,
            )

        def finish(unit, j):
            if unit not in result_tiles:
                result_tiles[unit] = norm_pool.tile([P, UNIT_TILES[unit], D], F32, name="result")
            nc.vector.scalar_tensor_tensor(
                out=result_tiles[unit][:, j, :], in0=scaled_tiles[unit][:, j, :], scalar=rstd_tiles[unit][:, j : j + 1],
                in1=beta_all, op0=ALU.mult, op1=ALU.add,
            )

        def store_tile(unit, j):
            b, rows = rows_of(unit)
            nc.sync.dma_start(out=out[b, rows.start + j * P : rows.start + (j + 1) * P, :], in_=result_tiles[unit][:, j, :])

        def store(unit):
            b, rows = rows_of(unit)
            nc.sync.dma_start(out=out[b, rows, :].rearrange("(p j) k -> p j k", j=UNIT_TILES[unit]), in_=result_tiles[unit][:])

        def live(unit):
            return 0 <= unit < UNITS

        for step in range(H * UNITS):
            i, h = divmod(step, H)
            if h == 0:
                if live(i + PREFETCH):
                    load_attn(i + PREFETCH, 0)
                    load_attn(i + PREFETCH, 1)
                if live(i + PREFETCH - RESID_LAG):
                    load_residual(i + PREFETCH - RESID_LAG)
                if live(i - 2):
                    second_head(i - 2)
                if live(i - 1):
                    quantise(i - 1, 1)
                if live(i - 4):
                    for j in range(UNIT_TILES[i - 4]):
                        finish(i - 4, j)
                if live(i - 4):
                    store(i - 4)
                if live(i - 3):
                    for j in range(UNIT_TILES[i - 3]):
                        take_mean(i - 3, j)
            else:
                if live(i - 1):
                    first_head(i - 1)
                if live(i):
                    quantise(i, 0)
                if live(i - 3):
                    for j in range(UNIT_TILES[i - 3]):
                        squares_of(i - 3, j)
                if live(i - 3):
                    for j in range(UNIT_TILES[i - 3]):
                        centre(i - 3, j)
            for j in range(MOST_TILES):
                flip(i, h, j)
                copy_out(i, h, j)
                if j == 0 and h == 1 and live(i - 3):
                    inverse_deviation(i - 3, 0, UNIT_TILES[i - 3])
            if h == 1 and live(i - 2):
                bring_back(i - 2)
            if live(i - 1):
                multiply(i - 1, h)
            if h == 1 and live(i + 1):
                if (i + 1) % 2 == 0 and 1 <= i < 12:
                    sort_words(i + 1, 1, 1, nc.vector.tensor_copy)
                if (i + 1) % 2 == 1 and 1 <= i < 12:
                    sort_words(i + 1, 1, 0, nc.scalar.copy)
            if step == CONSTANTS_STEP:
                spread_constants()

        last = UNITS - 1
        tiles = range(MOST_TILES)
        multiply(last, 0)
        quantise(last, 1)
        second_head(last - 1)
        multiply(last, 1)
        first_head(last)
        for j in tiles:
            take_mean(last - 2, j)
        for j in tiles:
            squares_of(last - 2, j)
        bring_back(last - 1)
        second_head(last)
        for j in tiles:
            finish(last - 3, j)
        store(last - 3)
        inverse_deviation(last - 2, 0, MOST_TILES)
        for j in tiles:
            take_mean(last - 1, j)
        bring_back(last)
        for j in tiles:
            squares_of(last - 1, j)
        for j in tiles:
            centre(last - 2, j)
        for j in tiles:
            finish(last - 2, j)
        store(last - 2)
        take_mean(last, 0)
        inverse_deviation(last - 1, 0, MOST_TILES)
        take_mean(last, 1)
        for j in tiles:
            squares_of(last, j)
        for j in tiles:
            centre(last - 1, j)
        for j in tiles:
            finish(last - 1, j)
        store(last - 1)
        for j in tiles:
            centre(last, j)
        for j in tiles:
            inverse_deviation(last, j, 1)
            finish(last, j)
            store_tile(last, j)
